import numpy as np
import ml_dtypes


def mxq(x, axis, fmt="e4m3"):
    dtype, down = {"e4m3": (ml_dtypes.float8_e4m3fn, 7), "e5m2": (ml_dtypes.float8_e5m2, 14)}[fmt]
    v = np.moveaxis(np.asarray(x, np.float32).astype(ml_dtypes.bfloat16).astype(np.float64), axis, -1)
    blocks = v.reshape(v.shape[:-1] + (-1, 32))
    amax = np.abs(blocks).max(-1, keepdims=True)
    byte = np.maximum(np.where(amax > 0, np.frexp(amax)[1] - 1 + 127, 0) - down, 1)
    scale = np.exp2(byte - 127.0)
    codes = (blocks / scale).astype(np.float32).astype(dtype).astype(np.float64)
    return np.moveaxis((codes * scale).reshape(v.shape), -1, axis)


WIDE = False


def mx_kscale(k):
    if not WIDE:
        return np.ones(k)
    levels = np.array([10, -10, 5, -5, 0])
    a = np.random.permutation(np.resize(levels, k // 512 * 4)).reshape(k // 512, 4)
    idx = np.arange(k)
    return np.exp2(a[idx // 512, idx % 128 // 32])


BF16 = ml_dtypes.bfloat16


def bf(x):
    return np.asarray(x, np.float32).astype(BF16)


def f64(x):
    return np.asarray(x).astype(np.float64)


B, A, E, H, NEXP, NACT = 128, 8, 512, 512, 8, 128
M = B * A


def sigmoid(v):
    return 1.0 / (1.0 + np.exp(-v))


def setup_inputs():
    s, t = mx_kscale(H), mx_kscale(H)
    return {
        "h": bf(np.random.standard_normal((M, H)) * 0.65 * s),
        "gate_logit": bf(np.random.standard_normal((M, NEXP))),
        "e_w1": bf(np.random.standard_normal((NEXP, H, H)) * 1.5 / np.sqrt(H) / s[None, None, :] * t[None, :, None]),
        "e_b1": bf(np.random.standard_normal((NEXP, H)) * 0.3 * t[None, :]),
        "e_w2": bf(np.random.standard_normal((NEXP, NACT, H)) * 2.0 / np.sqrt(H) / t[None, None, :]),
        "e_b2": bf(np.random.standard_normal((NEXP, NACT)) * 0.3),
    }


def reference(h, gate_logit, e_w1, e_b1, e_w2, e_b2):
    hq = mxq(f64(h), 1, "e4m3")
    h1 = np.maximum((hq @ mxq(f64(e_w1), 2, "e4m3").transpose(0, 2, 1)) + f64(e_b1)[:, None, :], 0.0)
    experts_out = (mxq(h1, 2, "e4m3") @ mxq(f64(e_w2), 2, "e4m3").transpose(0, 2, 1)) + f64(e_b2)[:, None, :]
    weight = sigmoid(f64(gate_logit))
    w = weight.T[:, :, None]
    final_q = (experts_out * w).mean(axis=0)
    return final_q, np.swapaxes(experts_out, 0, 1)

@@ -1,0 +1,338 @@
+from contextlib import ExitStack
+
+import concourse.bass as bass
+import concourse.mybir as mybir
+import concourse.tile as tile
+from concourse.masks import make_identity
+
+F32 = mybir.dt.float32
+BF16 = mybir.dt.bfloat16
+U32 = mybir.dt.uint32
+U8 = mybir.dt.uint8
+FP8X4 = mybir.dt.float8_e4m3fn_x4
+ACT = mybir.ActivationFunctionType
+ALU = mybir.AluOpType
+
+P = 128
+ROWS = 1024
+H = 512
+NACT = 128
+NEXP = 8
+MT = ROWS // P
+HALF_MT = 4
+UNITS = NEXP * 2
+
+FLOPS = 2 * ROWS * H * H * NEXP + 2 * ROWS * H * NACT * NEXP
+
+PINNED = False
+
+
+def tile_mspagent_pb_kernel(tc, h, gate_logit, e_w1, e_b1, e_w2, e_b2, out_0, out_1):
+    nc = tc.nc
+    with ExitStack() as ctx:
+        if PINNED:
+            ctx.enter_context(tc.manual_schedule())
+        keep = ctx.enter_context(tc.tile_pool(name="keep", bufs=1))
+        work = ctx.enter_context(tc.tile_pool(name="work", bufs=3))
+        ps_s1 = ctx.enter_context(tc.psum_pool(name="ps_s1", bufs=4))
+        ps_tp = ctx.enter_context(tc.psum_pool(name="ps_tp", bufs=2))
+        ps_s2 = ctx.enter_context(tc.psum_pool(name="ps_s2", bufs=2))
+
+        gl = keep.tile([P, MT * NEXP], BF16, name="gl")
+        nc.scalar.dma_start(out=gl[:], in_=gate_logit.rearrange("(p mt) x -> p (mt x)", mt=MT))
+        b1_rows = keep.tile([P, 256], BF16, name="b1_rows")
+        nc.vector.memset(b1_rows[:], 0.0)
+        nc.scalar.dma_start(out=b1_rows[0:16, :], in_=e_b1.rearrange("x (u c) -> (x u) c", u=2))
+        b2_rows = keep.tile([P, NEXP * NACT], BF16, name="b2_rows")
+        nc.vector.memset(b2_rows[:], 0.0)
+        nc.scalar.dma_start(out=b2_rows[0:1, :], in_=e_b2.rearrange("(o x) a -> o (x a)", o=1))
+
+        h_view = h.rearrange("(p mt) k -> p mt k", mt=MT)
+        h_sb = []
+        w1_sb = []
+        w2_sb = []
+        for half in range(2):
+            h_tile = keep.tile([P, HALF_MT, H], BF16, name="h_sb%d" % half)
+            h_sb.append(h_tile)
+        for ex in range(NEXP):
+            w1_tile = keep.tile([P, 2, 2, H], BF16, name="w1_sb%d" % ex)
+            w1_sb.append(w1_tile)
+        for q in range(2):
+            w2_tile = keep.tile([P, 4, H], BF16, name="w2_sb%d" % q)
+            w2_sb.append(w2_tile)
+
+        def load_h(half):
+            nc.sync.dma_start(out=h_sb[half][:], in_=h_view[:, half * HALF_MT:(half + 1) * HALF_MT, :])
+
+        def load_w1(ex):
+            nc.sync.dma_start(out=w1_sb[ex][:], in_=e_w1[ex].rearrange("(u p e) k -> p u e k", u=2, e=2))
+
+        def load_w2(q):
+            nc.sync.dma_start(out=w2_sb[q][:], in_=e_w2[4 * q:4 * q + 4].rearrange("x a k -> a x k"))
+
+        load_h(0)
+        load_w1(0)
+        load_h(1)
+        load_w2(0)
+        load_w1(1)
+        load_w1(2)
+        load_w2(1)
+        for ex in range(3, NEXP):
+            load_w1(ex)
+
+        ident = keep.tile([P, P], F32, name="ident")
+        make_identity(nc, ident[:])
+        ones = keep.tile([P, P], BF16, name="ones")
+        nc.vector.memset(ones[:], 1.0)
+
+        gate = keep.tile([P, MT * NEXP], F32, name="gate")
+        nc.scalar.activation(out=gate[:], in_=gl[:], func=ACT.Sigmoid)
+        nc.vector.tensor_scalar(out=gate[:], in0=gate[:], scalar1=1.0 / NEXP, scalar2=None, op0=ALU.mult)
+
+        b1_bank = ps_tp.tile([P, 2, 2, P], F32, name="b1_bank", tag="tp")
+        nc.tensor.transpose(b1_bank[:, 0, 0, :], b1_rows[:].bitcast(F32), ident[:])
+        b1T = keep.tile([P, 4 * NEXP], F32, name="b1T")
+        nc.vector.tensor_copy(out=b1T[:], in_=b1_bank[:, 0, 0, :].bitcast(BF16)[:, 0:4 * NEXP])
+
+        b2bc = keep.tile([P, NEXP * NACT], F32, name="b2bc")
+        for c in range(2):
+            b2_bank = ps_s2.tile([P, 512], F32, name="b2_bank", tag="s2")
+            nc.tensor.matmul(out=b2_bank[:], lhsT=ones[:], rhs=b2_rows[:, c * 512:(c + 1) * 512], start=True, stop=True)
+            nc.vector.tensor_copy(out=b2bc[:, c * 512:(c + 1) * 512], in_=b2_bank[:])
+
+        def t_bank(srcs):
+            bank = ps_tp.tile([P, 2, 2, P], F32, name="tp_bank", tag="tp")
+            for s in range(2):
+                words = srcs[s].bitcast(F32)
+                for u in range(2):
+                    nc.tensor.transpose(bank[:, s, u, :], words[:, u * P:(u + 1) * P], ident[:])
+            return bank
+
+        def x_bank(bank, grouped, engine):
+            dst = grouped.bitcast(F32).rearrange("p (s c u) -> p s c u", s=2, u=2)
+            src = bank[:].rearrange("p s u c -> p s c u")
+            if engine == "v":
+                nc.vector.tensor_copy(out=dst, in_=src)
+            else:
+                nc.scalar.copy(out=dst, in_=src)
+
+        def quantise(grouped, codes, scales):
+            nc.vector.quantize_mx(out=codes.bitcast(FP8X4), scales=scales, in_=grouped)
+
+        h_c = []
+        h_s = []
+        h_g = []
+        for half in range(2):
+            hg_tile = keep.tile([P, 512 * 4], BF16, name="h_g%d" % half, align_bytes=64)
+            hc_tile = keep.tile([P, 512], U32, name="h_c%d" % half, align_bytes=64)
+            hs_tile = keep.tile([P, 512], U8, name="h_s%d" % half, align_bytes=64)
+            h_g.append(hg_tile)
+            h_c.append(hc_tile)
+            h_s.append(hs_tile)
+        w1_g = {}
+        w1_c = {}
+        w1_s = {}
+        w2_g = {}
+        w2_c = {}
+        w2_s = {}
+
+        def srcs_of(kind, idx, b):
+            if kind == "h":
+                return [h_sb[idx][:, 2 * b + s, :] for s in range(2)]
+            if kind == "w1":
+                return [w1_sb[idx][:, b, s, :] for s in range(2)]
+            return [w2_sb[idx // 2][:, 2 * (idx % 2) + s, :] for s in range(2)]
+
+        def grouped_of(kind, idx, b):
+            if kind == "h":
+                return h_g[idx][:, b * 1024:(b + 1) * 1024]
+            if kind == "w1":
+                return w1_g[idx][:, b * 1024:(b + 1) * 1024]
+            return w2_g[idx][:]
+
+        def prep_alloc(kind, idx):
+            if kind == "w1":
+                g_tile = work.tile([P, 512 * 4], BF16, name="w1_g", tag="w1_g", bufs=2, align_bytes=64)
+                c_tile = work.tile([P, 512], U32, name="w1_c", tag="w1_c", align_bytes=64)
+                s_tile = work.tile([P, 512], U8, name="w1_s", tag="w1_s", align_bytes=64)
+                w1_g[idx] = g_tile
+                w1_c[idx] = c_tile
+                w1_s[idx] = s_tile
+            if kind == "w2":
+                g_tile = work.tile([P, 256 * 4], BF16, name="w2_g", tag="w2_g", bufs=2, align_bytes=64)
+                c_tile = keep.tile([P, 256], U32, name="w2_c%d" % idx, align_bytes=64)
+                s_tile = keep.tile([P, 256], U8, name="w2_s%d" % idx, align_bytes=64)
+                w2_g[idx] = g_tile
+                w2_c[idx] = c_tile
+                w2_s[idx] = s_tile
+
+        def prep_tx(kind, idx, engines):
+            prep_alloc(kind, idx)
+            banks = [t_bank(srcs_of(kind, idx, b)) for b in range(len(engines))]
+            return banks
+
+        def prep_x(kind, idx, engines, banks):
+            for b in range(len(engines)):
+                x_bank(banks[b], grouped_of(kind, idx, b), engines[b])
+
+        def prep_q(kind, idx):
+            if kind == "h":
+                quantise(h_g[idx][:], h_c[idx][:], h_s[idx][:])
+            elif kind == "w1":
+                quantise(w1_g[idx][:], w1_c[idx][:], w1_s[idx][:])
+            else:
+                quantise(w2_g[idx][:], w2_c[idx][:], w2_s[idx][:])
+
+        s1_banks = {}
+        planes = {}
+        h1_g = {}
+        h1_c = {}
+        h1_s = {}
+        s2_bank = {}
+        y_sb = {}
+        acc = []
+        for half in range(2):
+            acc_tile = keep.tile([P, HALF_MT, NACT], F32, name="acc%d" % half)
+            acc.append(acc_tile)
+        out1_view = out_1.rearrange("(p mt) x a -> p mt x a", mt=MT)
+        out0_view = out_0.rearrange("(p mt) a -> p mt a", mt=MT)
+
+        def mm1(n):
+            ex, half = n // 2, n % 2
+            banks = []
+            for t in range(4):
+                bank = ps_s1.tile([P, 512], F32, name="s1_bank", tag="s1")
+                nc.tensor.matmul_mx(
+                    out=bank[:],
+                    lhsT=w1_c[ex][:, t * P:(t + 1) * P].bitcast(FP8X4),
+                    lhsT_scale=w1_s[ex][:, t * P:(t + 1) * P],
+                    rhs=h_c[half][:].bitcast(FP8X4),
+                    rhs_scale=h_s[half][:],
+                    start=True,
+                    stop=True,
+                )
+                banks.append(bank)
+            s1_banks[n] = banks
+            pl_tile = work.tile([P, 4, 512], BF16, name="planes", tag="planes")
+            planes[n] = pl_tile
+
+        def c1(n, ts):
+            ex = n // 2
+            for t in ts:
+                nc.scalar.activation(
+                    out=planes[n][:, t, :],
+                    in_=s1_banks[n][t][:],
+                    func=ACT.Relu,
+                    bias=b1T[:, 4 * ex + t:4 * ex + t + 1],
+                    scale=1.0,
+                )
+
+        def regroup(n):
+            g_tile = work.tile([P, 512 * 4], BF16, name="h1_g", tag="h1_g", align_bytes=64)
+            h1_g[n] = g_tile
+            nc.vector.tensor_copy(
+                out=g_tile[:].rearrange("p (c i t) -> p c t i", i=4, t=4),
+                in_=planes[n][:].rearrange("p t (c i) -> p c t i", i=4),
+            )
+
+        def q1(n):
+            c_tile = work.tile([P, 512], U32, name="h1_c", tag="h1_c", align_bytes=64)
+            s_tile = work.tile([P, 512], U8, name="h1_s", tag="h1_s", align_bytes=64)
+            h1_c[n] = c_tile
+            h1_s[n] = s_tile
+            quantise(h1_g[n][:], c_tile[:], s_tile[:])
+
+        def mm2(n):
+            ex = n // 2
+            bank = ps_s2.tile([P, HALF_MT, NACT], F32, name="s2_bank", tag="s2")
+            s2_bank[n] = bank
+            lo = (ex % 2) * NACT
+            for i in range(HALF_MT):
+                nc.tensor.matmul_mx(
+                    out=bank[:, i, :],
+                    lhsT=h1_c[n][:, i * P:(i + 1) * P].bitcast(FP8X4),
+                    lhsT_scale=h1_s[n][:, i * P:(i + 1) * P],
+                    rhs=w2_c[ex // 2][:, lo:lo + NACT].bitcast(FP8X4),
+                    rhs_scale=w2_s[ex // 2][:, lo:lo + NACT],
+                    start=True,
+                    stop=True,
+                )
+
+        def add_b2(n):
+            ex = n // 2
+            y_tile = work.tile([P, HALF_MT, NACT], F32, name="y_sb", tag="y_sb", bufs=4)
+            y_sb[n] = y_tile
+            nc.vector.tensor_tensor(
+                out=y_tile[:],
+                in0=s2_bank[n][:],
+                in1=b2bc[:, ex * NACT:(ex + 1) * NACT].unsqueeze(1).to_broadcast([P, HALF_MT, NACT]),
+                op=ALU.add,
+            )
+
+        def gate_sum(n):
+            ex, half = n // 2, n % 2
+            for i in range(HALF_MT):
+                col = (half * HALF_MT + i) * NEXP + ex
+                if ex == 0:
+                    nc.vector.tensor_scalar(
+                        out=acc[half][:, i, :], in0=y_sb[n][:, i, :], scalar1=gate[:, col:col + 1], scalar2=None, op0=ALU.mult
+                    )
+                else:
+                    nc.vector.scalar_tensor_tensor(
+                        out=acc[half][:, i, :],
+                        in0=y_sb[n][:, i, :],
+                        scalar=gate[:, col:col + 1],
+                        in1=acc[half][:, i, :],
+                        op0=ALU.mult,
+                        op1=ALU.add,
+                    )
+
+        def store(n):
+            ex, half = n // 2, n % 2
+            nc.sync.dma_start(out=out1_view[:, half * HALF_MT:(half + 1) * HALF_MT, ex, :], in_=y_sb[n][:])
+            if ex == NEXP - 1:
+                nc.sync.dma_start(out=out0_view[:, half * HALF_MT:(half + 1) * HALF_MT, :], in_=acc[half][:])
+
+        for kind, idx, engines in (("h", 0, "vs"), ("w1", 0, "vs")):
+            banks = prep_tx(kind, idx, engines)
+            prep_x(kind, idx, engines, banks)
+            prep_q(kind, idx)
+
+        prep_plan = {
+            0: [("h", 1, "vv"), ("w1", 1, "vs")],
+            1: [("w2", 0, "v")],
+            2: [("w1", 2, "ss")],
+            3: [("w2", 1, "s")],
+            4: [("w1", 3, "ss")],
+            5: [("w2", 2, "s")],
+            6: [("w1", 4, "ss")],
+            7: [("w2", 3, "s")],
+            8: [("w1", 5, "ss")],
+            10: [("w1", 6, "ss")],
+            12: [("w1", 7, "ss")],
+        }
+
+        for k in range(UNITS + 2):
+            jobs = prep_plan.get(k, [])
+            if k < UNITS:
+                mm1(k)
+            if k < UNITS:
+                c1(k, (0, 1))
+            for kind, idx, engines in jobs:
+                banks = prep_tx(kind, idx, engines)
+                prep_x(kind, idx, engines, banks)
+            if k >= 2:
+                mm2(k - 2)
+            if k < UNITS:
+                c1(k, (2, 3))
+            if 1 <= k <= UNITS:
+                regroup(k - 1)
+            if k >= 2:
+                add_b2(k - 2)
+            if 1 <= k <= UNITS:
+                q1(k - 1)
+            if k >= 2:
+                gate_sum(k - 2)
+                store(k - 2)
+            for kind, idx, engines in jobs:
+                prep_q(kind, idx)

@@ -1,8 +1,6 @@
 from contextlib import ExitStack
 
-import concourse.bass as bass
 import concourse.mybir as mybir
-import concourse.tile as tile
 from concourse.masks import make_identity
 
 F32 = mybir.dt.float32
@@ -24,7 +22,9 @@ UNITS = NEXP * 2
 
 FLOPS = 2 * ROWS * H * H * NEXP + 2 * ROWS * H * NACT * NEXP
 
-PINNED = False
+PINNED = True
+S_COLS = [32, 32, 32, 32, 32, 32, 32, 32, 32, 32, 32, 32, 32, 64, 128, 256]
+V_PLANES = {}
 
 
 def tile_mspagent_pb_kernel(tc, h, gate_logit, e_w1, e_b1, e_w2, e_b2, out_0, out_1):
@@ -38,47 +38,62 @@ def tile_mspagent_pb_kernel(tc, h, gate_logit, e_w1, e_b1, e_w2, e_b2, out_0, ou
         ps_tp = ctx.enter_context(tc.psum_pool(name="ps_tp", bufs=2))
         ps_s2 = ctx.enter_context(tc.psum_pool(name="ps_s2", bufs=2))
 
-        gl = keep.tile([P, MT * NEXP], BF16, name="gl")
-        nc.scalar.dma_start(out=gl[:], in_=gate_logit.rearrange("(p mt) x -> p (mt x)", mt=MT))
         b1_rows = keep.tile([P, 256], BF16, name="b1_rows")
         nc.vector.memset(b1_rows[:], 0.0)
-        nc.scalar.dma_start(out=b1_rows[0:16, :], in_=e_b1.rearrange("x (u c) -> (x u) c", u=2))
         b2_rows = keep.tile([P, NEXP * NACT], BF16, name="b2_rows")
         nc.vector.memset(b2_rows[:], 0.0)
-        nc.scalar.dma_start(out=b2_rows[0:1, :], in_=e_b2.rearrange("(o x) a -> o (x a)", o=1))
+        gl = keep.tile([P, MT * NEXP], BF16, name="gl")
+        nc.sync.dma_start(out=gl[:], in_=gate_logit.rearrange("(p mt) x -> p (mt x)", mt=MT))
+        nc.sync.dma_start(out=b1_rows[0:16, :], in_=e_b1.rearrange("x (u c) -> (x u) c", u=2))
+        nc.sync.dma_start(out=b2_rows[0:1, :], in_=e_b2.rearrange("(o x) a -> o (x a)", o=1))
 
         h_view = h.rearrange("(p mt) k -> p mt k", mt=MT)
         h_sb = []
         w1_sb = []
         w2_sb = []
-        for half in range(2):
-            h_tile = keep.tile([P, HALF_MT, H], BF16, name="h_sb%d" % half)
+        for q in range(4):
+            h_tile = keep.tile([P, 2, H], BF16, name="h_sb%d" % q)
             h_sb.append(h_tile)
         for ex in range(NEXP):
-            w1_tile = keep.tile([P, 2, 2, H], BF16, name="w1_sb%d" % ex)
-            w1_sb.append(w1_tile)
-        for q in range(2):
-            w2_tile = keep.tile([P, 4, H], BF16, name="w2_sb%d" % q)
+            for u in range(2):
+                w1_tile = keep.tile([P, 2, H], BF16, name="w1_sb%d_%d" % (ex, u))
+                w1_sb.append(w1_tile)
+        for q in range(4):
+            w2_tile = keep.tile([P, 2, H], BF16, name="w2_sb%d" % q)
             w2_sb.append(w2_tile)
 
-        def load_h(half):
-            nc.sync.dma_start(out=h_sb[half][:], in_=h_view[:, half * HALF_MT:(half + 1) * HALF_MT, :])
+        def load_h(q):
+            nc.sync.dma_start(out=h_sb[q][:], in_=h_view[:, 2 * q:2 * q + 2, :])
 
-        def load_w1(ex):
-            nc.sync.dma_start(out=w1_sb[ex][:], in_=e_w1[ex].rearrange("(u p e) k -> p u e k", u=2, e=2))
+        def load_w1(ex, u):
+            nc.sync.dma_start(
+                out=w1_sb[2 * ex + u][:], in_=e_w1[ex, 256 * u:256 * u + 256, :].rearrange("(p e) k -> p e k", e=2)
+            )
 
         def load_w2(q):
-            nc.sync.dma_start(out=w2_sb[q][:], in_=e_w2[4 * q:4 * q + 4].rearrange("x a k -> a x k"))
+            nc.sync.dma_start(out=w2_sb[q][:], in_=e_w2[2 * q:2 * q + 2].rearrange("x a k -> a x k"))
 
         load_h(0)
-        load_w1(0)
         load_h(1)
+        load_w1(0, 0)
+        load_w1(0, 1)
+        load_h(2)
+        load_h(3)
+        load_w1(1, 0)
+        load_w1(1, 1)
         load_w2(0)
-        load_w1(1)
-        load_w1(2)
+        load_w1(2, 0)
+        load_w1(2, 1)
         load_w2(1)
-        for ex in range(3, NEXP):
-            load_w1(ex)
+        load_w1(3, 0)
+        load_w1(3, 1)
+        load_w2(2)
+        load_w1(4, 0)
+        load_w1(4, 1)
+        load_w2(3)
+        for ex in range(5, NEXP):
+            load_w1(ex, 0)
+            load_w1(ex, 1)
 
         ident = keep.tile([P, P], F32, name="ident")
         make_identity(nc, ident[:])
@@ -89,21 +104,28 @@ def tile_mspagent_pb_kernel(tc, h, gate_logit, e_w1, e_b1, e_w2, e_b2, out_0, ou
         nc.scalar.activation(out=gate[:], in_=gl[:], func=ACT.Sigmoid)
         nc.vector.tensor_scalar(out=gate[:], in0=gate[:], scalar1=1.0 / NEXP, scalar2=None, op0=ALU.mult)
 
-        b1_bank = ps_tp.tile([P, 2, 2, P], F32, name="b1_bank", tag="tp")
-        nc.tensor.transpose(b1_bank[:, 0, 0, :], b1_rows[:].bitcast(F32), ident[:])
+        b1_bank = ps_s2.tile([P, 512], F32, name="b1_bank", tag="s2")
+        nc.tensor.transpose(b1_bank[:, 0:P], b1_rows[:].bitcast(F32), ident[:])
         b1T = keep.tile([P, 4 * NEXP], F32, name="b1T")
-        nc.vector.tensor_copy(out=b1T[:], in_=b1_bank[:, 0, 0, :].bitcast(BF16)[:, 0:4 * NEXP])
+        nc.vector.tensor_copy(out=b1T[:], in_=b1_bank[:, 0:P].bitcast(BF16)[:, 0:4 * NEXP])
 
         b2bc = keep.tile([P, NEXP * NACT], F32, name="b2bc")
-        for c in range(2):
+
+        def spread_b2(c, engine):
             b2_bank = ps_s2.tile([P, 512], F32, name="b2_bank", tag="s2")
             nc.tensor.matmul(out=b2_bank[:], lhsT=ones[:], rhs=b2_rows[:, c * 512:(c + 1) * 512], start=True, stop=True)
-            nc.vector.tensor_copy(out=b2bc[:, c * 512:(c + 1) * 512], in_=b2_bank[:])
+            if engine == "v":
+                nc.vector.tensor_copy(out=b2bc[:, c * 512:(c + 1) * 512], in_=b2_bank[:])
+            else:
+                nc.scalar.copy(out=b2bc[:, c * 512:(c + 1) * 512], in_=b2_bank[:])
 
-        def t_bank(srcs):
-            bank = ps_tp.tile([P, 2, 2, P], F32, name="tp_bank", tag="tp")
+        def t_bank(src_tile, pool_tag):
+            if pool_tag == "s1":
+                bank = ps_s1.tile([P, 2, 2, P], F32, name="tp_bank1", tag="s1")
+            else:
+                bank = ps_tp.tile([P, 2, 2, P], F32, name="tp_bank", tag="tp")
             for s in range(2):
-                words = srcs[s].bitcast(F32)
+                words = src_tile[:, s, :].bitcast(F32)
                 for u in range(2):
                     nc.tensor.transpose(bank[:, s, u, :], words[:, u * P:(u + 1) * P], ident[:])
             return bank
@@ -119,69 +141,50 @@ def tile_mspagent_pb_kernel(tc, h, gate_logit, e_w1, e_b1, e_w2, e_b2, out_0, ou
         def quantise(grouped, codes, scales):
             nc.vector.quantize_mx(out=codes.bitcast(FP8X4), scales=scales, in_=grouped)
 
-        h_c = []
-        h_s = []
-        h_g = []
+        grp = {}
+        cod = {}
+        sca = {}
         for half in range(2):
-            hg_tile = keep.tile([P, 512 * 4], BF16, name="h_g%d" % half, align_bytes=64)
-            hc_tile = keep.tile([P, 512], U32, name="h_c%d" % half, align_bytes=64)
-            hs_tile = keep.tile([P, 512], U8, name="h_s%d" % half, align_bytes=64)
-            h_g.append(hg_tile)
-            h_c.append(hc_tile)
-            h_s.append(hs_tile)
-        w1_g = {}
-        w1_c = {}
-        w1_s = {}
-        w2_g = {}
-        w2_c = {}
-        w2_s = {}
+            g_tile = keep.tile([P, 512 * 4], BF16, name="h_g%d" % half, align_bytes=64)
+            c_tile = keep.tile([P, 512], U32, name="h_c%d" % half, align_bytes=64)
+            s_tile = keep.tile([P, 512], U8, name="h_s%d" % half, align_bytes=64)
+            grp[("h", half)] = g_tile
+            cod[("h", half)] = c_tile
+            sca[("h", half)] = s_tile
+        for ex in range(NEXP):
+            c_tile = keep.tile([P, 512], U32, name="w1_c%d" % ex, align_bytes=64)
+            s_tile = keep.tile([P, 512], U8, name="w1_s%d" % ex, align_bytes=64)
+            cod[("w1", ex)] = c_tile
+            sca[("w1", ex)] = s_tile
+        for q in range(4):
+            c_tile = keep.tile([P, 256], U32, name="w2_c%d" % q, align_bytes=64)
+            s_tile = keep.tile([P, 256], U8, name="w2_s%d" % q, align_bytes=64)
+            cod[("w2", q)] = c_tile
+            sca[("w2", q)] = s_tile
+        live_banks = {}
 
-        def srcs_of(kind, idx, b):
-            if kind == "h":
-                return [h_sb[idx][:, 2 * b + s, :] for s in range(2)]
-            if kind == "w1":
-                return [w1_sb[idx][:, b, s, :] for s in range(2)]
-            return [w2_sb[idx // 2][:, 2 * (idx % 2) + s, :] for s in range(2)]
-
-        def grouped_of(kind, idx, b):
-            if kind == "h":
-                return h_g[idx][:, b * 1024:(b + 1) * 1024]
-            if kind == "w1":
-                return w1_g[idx][:, b * 1024:(b + 1) * 1024]
-            return w2_g[idx][:]
-
-        def prep_alloc(kind, idx):
-            if kind == "w1":
-                g_tile = work.tile([P, 512 * 4], BF16, name="w1_g", tag="w1_g", bufs=2, align_bytes=64)
-                c_tile = work.tile([P, 512], U32, name="w1_c", tag="w1_c", align_bytes=64)
-                s_tile = work.tile([P, 512], U8, name="w1_s", tag="w1_s", align_bytes=64)
-                w1_g[idx] = g_tile
-                w1_c[idx] = c_tile
-                w1_s[idx] = s_tile
+        def job_t(kind, idx, b, pool_tag="tp"):
+            if kind == "w1" and b == 0:
+                g_tile = work.tile([P, 512 * 4], BF16, name="w1_g", tag="w1_g", align_bytes=64)
+                grp[(kind, idx)] = g_tile
             if kind == "w2":
                 g_tile = work.tile([P, 256 * 4], BF16, name="w2_g", tag="w2_g", bufs=2, align_bytes=64)
-                c_tile = keep.tile([P, 256], U32, name="w2_c%d" % idx, align_bytes=64)
-                s_tile = keep.tile([P, 256], U8, name="w2_s%d" % idx, align_bytes=64)
-                w2_g[idx] = g_tile
-                w2_c[idx] = c_tile
-                w2_s[idx] = s_tile
-
-        def prep_tx(kind, idx, engines):
-            prep_alloc(kind, idx)
-            banks = [t_bank(srcs_of(kind, idx, b)) for b in range(len(engines))]
-            return banks
-
-        def prep_x(kind, idx, engines, banks):
-            for b in range(len(engines)):
-                x_bank(banks[b], grouped_of(kind, idx, b), engines[b])
-
-        def prep_q(kind, idx):
+                grp[(kind, idx)] = g_tile
             if kind == "h":
-                quantise(h_g[idx][:], h_c[idx][:], h_s[idx][:])
+                src_tile = h_sb[2 * idx + b]
             elif kind == "w1":
-                quantise(w1_g[idx][:], w1_c[idx][:], w1_s[idx][:])
+                src_tile = w1_sb[2 * idx + b]
             else:
-                quantise(w2_g[idx][:], w2_c[idx][:], w2_s[idx][:])
+                src_tile = w2_sb[idx]
+            live_banks[(kind, idx, b)] = t_bank(src_tile, pool_tag)
+
+        def job_x(kind, idx, b, engine):
+            x_bank(live_banks[(kind, idx, b)], grp[(kind, idx)][:, b * 1024:(b + 1) * 1024], engine)
+
+        def job_q(kind, idx, lo=0, hi=None):
+            width = cod[(kind, idx)].shape[1]
+            top = width if hi is None else hi
+            quantise(grp[(kind, idx)][:, 4 * lo:4 * top], cod[(kind, idx)][:, lo:top], sca[(kind, idx)][:, lo:top])
 
         s1_banks = {}
         planes = {}
@@ -197,63 +200,71 @@ def tile_mspagent_pb_kernel(tc, h, gate_logit, e_w1, e_b1, e_w2, e_b2, out_0, ou
         out1_view = out_1.rearrange("(p mt) x a -> p mt x a", mt=MT)
         out0_view = out_0.rearrange("(p mt) a -> p mt a", mt=MT)
 
-        def mm1(n):
+        def mm1(n, ts=(0, 1, 2, 3)):
             ex, half = n // 2, n % 2
-            banks = []
-            for t in range(4):
+            if n not in s1_banks:
+                s1_banks[n] = {}
+                pl_tile = work.tile([P, 4, 512], BF16, name="planes", tag="planes")
+                planes[n] = pl_tile
+            for t in ts:
                 bank = ps_s1.tile([P, 512], F32, name="s1_bank", tag="s1")
                 nc.tensor.matmul_mx(
                     out=bank[:],
-                    lhsT=w1_c[ex][:, t * P:(t + 1) * P].bitcast(FP8X4),
-                    lhsT_scale=w1_s[ex][:, t * P:(t + 1) * P],
-                    rhs=h_c[half][:].bitcast(FP8X4),
-                    rhs_scale=h_s[half][:],
+                    lhsT=cod[("w1", ex)][:, t * P:(t + 1) * P].bitcast(FP8X4),
+                    lhsT_scale=sca[("w1", ex)][:, t * P:(t + 1) * P],
+                    rhs=cod[("h", half)][:].bitcast(FP8X4),
+                    rhs_scale=sca[("h", half)][:],
                     start=True,
                     stop=True,
                 )
-                banks.append(bank)
-            s1_banks[n] = banks
-            pl_tile = work.tile([P, 4, 512], BF16, name="planes", tag="planes")
-            planes[n] = pl_tile
+                s1_banks[n][t] = bank
 
-        def c1(n, ts):
+        def c1(n, t):
             ex = n // 2
-            for t in ts:
-                nc.scalar.activation(
-                    out=planes[n][:, t, :],
-                    in_=s1_banks[n][t][:],
-                    func=ACT.Relu,
-                    bias=b1T[:, 4 * ex + t:4 * ex + t + 1],
-                    scale=1.0,
+            bias = b1T[:, 4 * ex + t:4 * ex + t + 1]
+            if t in V_PLANES.get(n, ()):
+                nc.vector.tensor_scalar(
+                    out=planes[n][:, t, :], in0=s1_banks[n][t][:], scalar1=bias, scalar2=0.0, op0=ALU.add, op1=ALU.max
                 )
+            else:
+                nc.scalar.activation(out=planes[n][:, t, :], in_=s1_banks[n][t][:], func=ACT.Relu, bias=bias, scale=1.0)
 
-        def regroup(n):
-            g_tile = work.tile([P, 512 * 4], BF16, name="h1_g", tag="h1_g", align_bytes=64)
-            h1_g[n] = g_tile
-            nc.vector.tensor_copy(
-                out=g_tile[:].rearrange("p (c i t) -> p c t i", i=4, t=4),
-                in_=planes[n][:].rearrange("p t (c i) -> p c t i", i=4),
-            )
+        def regroup(n, engine):
+            if n not in h1_g:
+                g_tile = work.tile([P, 512 * 4], BF16, name="h1_g", tag="h1_g", align_bytes=64)
+                h1_g[n] = g_tile
+            cut = 512 - S_COLS[n]
+            lo, hi = (0, cut) if engine == "v" else (cut, 512)
+            if lo == hi:
+                return
+            dst = h1_g[n][:, 4 * lo:4 * hi].rearrange("p (c i t) -> p c t i", i=4, t=4)
+            src = planes[n][:, :, lo:hi].rearrange("p t (c i) -> p c t i", i=4)
+            if engine == "v":
+                nc.vector.tensor_copy(out=dst, in_=src)
+            else:
+                nc.scalar.copy(out=dst, in_=src)
 
-        def q1(n):
-            c_tile = work.tile([P, 512], U32, name="h1_c", tag="h1_c", align_bytes=64)
-            s_tile = work.tile([P, 512], U8, name="h1_s", tag="h1_s", align_bytes=64)
-            h1_c[n] = c_tile
-            h1_s[n] = s_tile
-            quantise(h1_g[n][:], c_tile[:], s_tile[:])
+        def q1(n, lo=0, hi=512):
+            if n not in h1_c:
+                c_tile = work.tile([P, 512], U32, name="h1_c", tag="h1_c", align_bytes=64)
+                s_tile = work.tile([P, 512], U8, name="h1_s", tag="h1_s", align_bytes=64)
+                h1_c[n] = c_tile
+                h1_s[n] = s_tile
+            quantise(h1_g[n][:, 4 * lo:4 * hi], h1_c[n][:, lo:hi], h1_s[n][:, lo:hi])
 
-        def mm2(n):
+        def mm2(n, tiles=(0, 1, 2, 3)):
             ex = n // 2
-            bank = ps_s2.tile([P, HALF_MT, NACT], F32, name="s2_bank", tag="s2")
-            s2_bank[n] = bank
+            if n not in s2_bank:
+                bank = ps_s2.tile([P, HALF_MT, NACT], F32, name="s2_bank", tag="s2")
+                s2_bank[n] = bank
             lo = (ex % 2) * NACT
-            for i in range(HALF_MT):
+            for i in tiles:
                 nc.tensor.matmul_mx(
-                    out=bank[:, i, :],
+                    out=s2_bank[n][:, i, :],
                     lhsT=h1_c[n][:, i * P:(i + 1) * P].bitcast(FP8X4),
                     lhsT_scale=h1_s[n][:, i * P:(i + 1) * P],
-                    rhs=w2_c[ex // 2][:, lo:lo + NACT].bitcast(FP8X4),
-                    rhs_scale=w2_s[ex // 2][:, lo:lo + NACT],
+                    rhs=cod[("w2", ex // 2)][:, lo:lo + NACT].bitcast(FP8X4),
+                    rhs_scale=sca[("w2", ex // 2)][:, lo:lo + NACT],
                     start=True,
                     stop=True,
                 )
@@ -293,14 +304,35 @@ def tile_mspagent_pb_kernel(tc, h, gate_logit, e_w1, e_b1, e_w2, e_b2, out_0, ou
             if ex == NEXP - 1:
                 nc.sync.dma_start(out=out0_view[:, half * HALF_MT:(half + 1) * HALF_MT, :], in_=acc[half][:])
 
-        for kind, idx, engines in (("h", 0, "vs"), ("w1", 0, "vs")):
-            banks = prep_tx(kind, idx, engines)
-            prep_x(kind, idx, engines, banks)
-            prep_q(kind, idx)
+        job_t("h", 0, 0)
+        job_t("h", 0, 1)
+        job_x("h", 0, 0, "v")
+        job_x("h", 0, 1, "s")
+        job_t("w1", 0, 0)
+        job_t("w1", 0, 1)
+        job_q("h", 0, 0, 256)
+        job_x("w1", 0, 0, "v")
+        job_x("w1", 0, 1, "s")
+        job_q("h", 0, 256, 512)
+        job_q("w1", 0, 0, 256)
+        job_q("w1", 0, 256, 512)
+        job_t("h", 1, 0)
+        mm1(0, (0, 1))
+        job_t("h", 1, 1)
+        mm1(0, (2, 3))
+        job_x("h", 1, 0, "v")
+        job_x("h", 1, 1, "v")
+        job_q("h", 1)
+        for t in range(4):
+            c1(0, t)
+        regroup(0, "s")
+        job_t("w1", 1, 0)
+        job_t("w1", 1, 1)
+        job_x("w1", 1, 0, "v")
+        job_x("w1", 1, 1, "v")
 
         prep_plan = {
-            0: [("h", 1, "vv"), ("w1", 1, "vs")],
-            1: [("w2", 0, "v")],
+            1: [("b2", 0, "ss")],
             2: [("w1", 2, "ss")],
             3: [("w2", 1, "s")],
             4: [("w1", 3, "ss")],
@@ -312,27 +344,40 @@ def tile_mspagent_pb_kernel(tc, h, gate_logit, e_w1, e_b1, e_w2, e_b2, out_0, ou
             12: [("w1", 7, "ss")],
         }
 
-        for k in range(UNITS + 2):
+        for k in range(1, UNITS + 2):
             jobs = prep_plan.get(k, [])
             if k < UNITS:
                 mm1(k)
-            if k < UNITS:
-                c1(k, (0, 1))
-            for kind, idx, engines in jobs:
-                banks = prep_tx(kind, idx, engines)
-                prep_x(kind, idx, engines, banks)
             if k >= 2:
                 mm2(k - 2)
             if k < UNITS:
-                c1(k, (2, 3))
+                for t in range(4):
+                    c1(k, t)
+                regroup(k, "s")
+            for kind, idx, engines in jobs:
+                if kind == "b2":
+                    spread_b2(0, engines[0])
+                    spread_b2(1, engines[1])
+                else:
+                    for b in range(len(engines)):
+                        job_t(kind, idx, b)
+                    for b in range(len(engines)):
+                        job_x(kind, idx, b, engines[b])
             if 1 <= k <= UNITS:
-                regroup(k - 1)
+                regroup(k - 1, "v")
+            if k == 1:
+                job_q("w1", 1)
+                job_t("w2", 0, 0)
+                job_x("w2", 0, 0, "v")
+            for kind, idx, engines in prep_plan.get(k - 1, []):
+                if kind != "b2":
+                    job_q(kind, idx)
             if k >= 2:
                 add_b2(k - 2)
             if 1 <= k <= UNITS:
                 q1(k - 1)
+            if k == 1:
+                job_q("w2", 0)
             if k >= 2:
                 gate_sum(k - 2)
                 store(k - 2)
-            for kind, idx, engines in jobs:
-                prep_q(kind, idx)

@@ -22,7 +22,7 @@ UNITS = NEXP * 2
 
 FLOPS = 2 * ROWS * H * H * NEXP + 2 * ROWS * H * NACT * NEXP
 
-PINNED = True
+PINNED = False
 S_COLS = [32, 32, 32, 32, 32, 32, 32, 32, 32, 32, 32, 32, 32, 64, 128, 256]
 V_PLANES = {}
 

@@ -12,372 +12,197 @@ ACT = mybir.ActivationFunctionType
 ALU = mybir.AluOpType
 
 P = 128
+PACK = 4
 ROWS = 1024
-H = 512
-NACT = 128
-NEXP = 8
-MT = ROWS // P
-HALF_MT = 4
-UNITS = NEXP * 2
+HID = 512
+ACTIONS = 128
+EXPERTS = 8
+ROW_TILES = ROWS // P
+HALF_TILES = ROW_TILES // 2
+HALF_ROWS = ROWS // 2
+UNITS = 2 * EXPERTS
 
-FLOPS = 2 * ROWS * H * H * NEXP + 2 * ROWS * H * NACT * NEXP
+FLOPS = 2 * ROWS * HID * HID * EXPERTS + 2 * ROWS * HID * ACTIONS * EXPERTS
 
-PINNED = False
-S_COLS = [32, 32, 32, 32, 32, 32, 32, 32, 32, 32, 32, 32, 32, 64, 128, 256]
-V_PLANES = {}
+
+def scalar_share(unit):
+    return 32 * 2 ** max(0, unit - (UNITS - 4))
 
 
 def tile_mspagent_pb_kernel(tc, h, gate_logit, e_w1, e_b1, e_w2, e_b2, out_0, out_1):
     nc = tc.nc
     with ExitStack() as ctx:
-        if PINNED:
-            ctx.enter_context(tc.manual_schedule())
-        keep = ctx.enter_context(tc.tile_pool(name="keep", bufs=1))
-        work = ctx.enter_context(tc.tile_pool(name="work", bufs=3))
-        ps_s1 = ctx.enter_context(tc.psum_pool(name="ps_s1", bufs=4))
-        ps_tp = ctx.enter_context(tc.psum_pool(name="ps_tp", bufs=2))
-        ps_s2 = ctx.enter_context(tc.psum_pool(name="ps_s2", bufs=2))
+        resident = ctx.enter_context(tc.tile_pool(name="resident", bufs=1))
+        rotating = ctx.enter_context(tc.tile_pool(name="rotating", bufs=3))
+        psum_planes = ctx.enter_context(tc.psum_pool(name="psum_planes", bufs=4))
+        psum_transposes = ctx.enter_context(tc.psum_pool(name="psum_transposes", bufs=2))
+        psum_stage2 = ctx.enter_context(tc.psum_pool(name="psum_stage2", bufs=2))
 
-        b1_rows = keep.tile([P, 256], BF16, name="b1_rows")
+        gate_logits = resident.tile([P, ROW_TILES * EXPERTS], BF16, name="gate_logits")
+        nc.sync.dma_start(out=gate_logits[:], in_=gate_logit.rearrange("(p r) x -> p (r x)", r=ROW_TILES))
+        b1_rows = resident.tile([P, 2 * P], BF16, name="b1_rows")
         nc.vector.memset(b1_rows[:], 0.0)
-        b2_rows = keep.tile([P, NEXP * NACT], BF16, name="b2_rows")
-        nc.vector.memset(b2_rows[:], 0.0)
-        gl = keep.tile([P, MT * NEXP], BF16, name="gl")
-        nc.sync.dma_start(out=gl[:], in_=gate_logit.rearrange("(p mt) x -> p (mt x)", mt=MT))
-        nc.sync.dma_start(out=b1_rows[0:16, :], in_=e_b1.rearrange("x (u c) -> (x u) c", u=2))
-        nc.sync.dma_start(out=b2_rows[0:1, :], in_=e_b2.rearrange("(o x) a -> o (x a)", o=1))
+        nc.sync.dma_start(out=b1_rows[0:2 * EXPERTS, :], in_=e_b1.rearrange("x (u c) -> (x u) c", u=2))
 
-        h_view = h.rearrange("(p mt) k -> p mt k", mt=MT)
-        h_sb = []
-        w1_sb = []
-        w2_sb = []
-        for q in range(4):
-            h_tile = keep.tile([P, 2, H], BF16, name="h_sb%d" % q)
-            h_sb.append(h_tile)
-        for ex in range(NEXP):
-            for u in range(2):
-                w1_tile = keep.tile([P, 2, H], BF16, name="w1_sb%d_%d" % (ex, u))
-                w1_sb.append(w1_tile)
-        for q in range(4):
-            w2_tile = keep.tile([P, 2, H], BF16, name="w2_sb%d" % q)
-            w2_sb.append(w2_tile)
+        def load_pair(name, view):
+            pair = resident.tile([P, 2, HID], BF16, name=name)
+            nc.sync.dma_start(out=pair[:], in_=view)
+            return pair
 
-        def load_h(q):
-            nc.sync.dma_start(out=h_sb[q][:], in_=h_view[:, 2 * q:2 * q + 2, :])
+        def load_h(half):
+            view = h.rearrange("(p r) k -> p r k", r=ROW_TILES)
+            first = half * HALF_TILES
+            return [load_pair("h_%d_%d" % (half, b), view[:, first + 2 * b:first + 2 * b + 2, :]) for b in range(2)]
 
-        def load_w1(ex, u):
-            nc.sync.dma_start(
-                out=w1_sb[2 * ex + u][:], in_=e_w1[ex, 256 * u:256 * u + 256, :].rearrange("(p e) k -> p e k", e=2)
-            )
+        def load_w1(x):
+            return [
+                load_pair("w1_%d_%d" % (x, u), e_w1[x, 2 * P * u:2 * P * (u + 1), :].rearrange("(p e) k -> p e k", e=2))
+                for u in range(2)
+            ]
 
-        def load_w2(q):
-            nc.sync.dma_start(out=w2_sb[q][:], in_=e_w2[2 * q:2 * q + 2].rearrange("x a k -> a x k"))
+        def load_w2(pair_of_experts):
+            first = 2 * pair_of_experts
+            return [load_pair("w2_%d" % pair_of_experts, e_w2[first:first + 2].rearrange("x a k -> a x k"))]
 
-        load_h(0)
-        load_h(1)
-        load_w1(0, 0)
-        load_w1(0, 1)
-        load_h(2)
-        load_h(3)
-        load_w1(1, 0)
-        load_w1(1, 1)
-        load_w2(0)
-        load_w1(2, 0)
-        load_w1(2, 1)
-        load_w2(1)
-        load_w1(3, 0)
-        load_w1(3, 1)
-        load_w2(2)
-        load_w1(4, 0)
-        load_w1(4, 1)
-        load_w2(3)
-        for ex in range(5, NEXP):
-            load_w1(ex, 0)
-            load_w1(ex, 1)
+        h_raw = {}
+        w1_raw = {}
+        w2_raw = {}
+        h_raw[0] = load_h(0)
+        w1_raw[0] = load_w1(0)
+        h_raw[1] = load_h(1)
+        w1_raw[1] = load_w1(1)
+        w2_raw[0] = load_w2(0)
+        b2_all = resident.tile([P, EXPERTS * ACTIONS], BF16, name="b2_all")
+        nc.sync.dma_start(out=b2_all[:], in_=e_b2.rearrange("x a -> (x a)").partition_broadcast(P))
+        for x in range(2, EXPERTS):
+            w1_raw[x] = load_w1(x)
+            if x - 1 < EXPERTS // 2:
+                w2_raw[x - 1] = load_w2(x - 1)
 
-        ident = keep.tile([P, P], F32, name="ident")
-        make_identity(nc, ident[:])
-        ones = keep.tile([P, P], BF16, name="ones")
-        nc.vector.memset(ones[:], 1.0)
+        identity = resident.tile([P, P], F32, name="identity")
+        make_identity(nc, identity[:])
 
-        gate = keep.tile([P, MT * NEXP], F32, name="gate")
-        nc.scalar.activation(out=gate[:], in_=gl[:], func=ACT.Sigmoid)
-        nc.vector.tensor_scalar(out=gate[:], in0=gate[:], scalar1=1.0 / NEXP, scalar2=None, op0=ALU.mult)
+        gate = resident.tile([P, ROW_TILES * EXPERTS], F32, name="gate")
+        nc.scalar.activation(out=gate[:], in_=gate_logits[:], func=ACT.Sigmoid)
+        nc.vector.tensor_scalar(out=gate[:], in0=gate[:], scalar1=1.0 / EXPERTS, scalar2=None, op0=ALU.mult)
 
-        b1_bank = ps_s2.tile([P, 512], F32, name="b1_bank", tag="s2")
-        nc.tensor.transpose(b1_bank[:, 0:P], b1_rows[:].bitcast(F32), ident[:])
-        b1T = keep.tile([P, 4 * NEXP], F32, name="b1T")
-        nc.vector.tensor_copy(out=b1T[:], in_=b1_bank[:, 0:P].bitcast(BF16)[:, 0:4 * NEXP])
+        b1_bank = psum_transposes.tile([P, 2, 2, P], F32, name="b1_bank", tag="bank")
+        nc.tensor.transpose(b1_bank[:, 0, 0, :], b1_rows[:].bitcast(F32), identity[:])
+        b1 = resident.tile([P, PACK * EXPERTS], F32, name="b1")
+        nc.vector.tensor_copy(out=b1[:], in_=b1_bank[:, 0, 0, :].bitcast(BF16)[:, 0:PACK * EXPERTS])
 
-        b2bc = keep.tile([P, NEXP * NACT], F32, name="b2bc")
-
-        def spread_b2(c, engine):
-            b2_bank = ps_s2.tile([P, 512], F32, name="b2_bank", tag="s2")
-            nc.tensor.matmul(out=b2_bank[:], lhsT=ones[:], rhs=b2_rows[:, c * 512:(c + 1) * 512], start=True, stop=True)
-            if engine == "v":
-                nc.vector.tensor_copy(out=b2bc[:, c * 512:(c + 1) * 512], in_=b2_bank[:])
-            else:
-                nc.scalar.copy(out=b2bc[:, c * 512:(c + 1) * 512], in_=b2_bank[:])
-
-        def t_bank(src_tile, pool_tag):
-            if pool_tag == "s1":
-                bank = ps_s1.tile([P, 2, 2, P], F32, name="tp_bank1", tag="s1")
-            else:
-                bank = ps_tp.tile([P, 2, 2, P], F32, name="tp_bank", tag="tp")
-            for s in range(2):
-                words = src_tile[:, s, :].bitcast(F32)
-                for u in range(2):
-                    nc.tensor.transpose(bank[:, s, u, :], words[:, u * P:(u + 1) * P], ident[:])
-            return bank
-
-        def x_bank(bank, grouped, engine):
-            dst = grouped.bitcast(F32).rearrange("p (s c u) -> p s c u", s=2, u=2)
-            src = bank[:].rearrange("p s u c -> p s c u")
-            if engine == "v":
-                nc.vector.tensor_copy(out=dst, in_=src)
-            else:
-                nc.scalar.copy(out=dst, in_=src)
-
-        def quantise(grouped, codes, scales):
-            nc.vector.quantize_mx(out=codes.bitcast(FP8X4), scales=scales, in_=grouped)
-
-        grp = {}
-        cod = {}
-        sca = {}
-        for half in range(2):
-            g_tile = keep.tile([P, 512 * 4], BF16, name="h_g%d" % half, align_bytes=64)
-            c_tile = keep.tile([P, 512], U32, name="h_c%d" % half, align_bytes=64)
-            s_tile = keep.tile([P, 512], U8, name="h_s%d" % half, align_bytes=64)
-            grp[("h", half)] = g_tile
-            cod[("h", half)] = c_tile
-            sca[("h", half)] = s_tile
-        for ex in range(NEXP):
-            c_tile = keep.tile([P, 512], U32, name="w1_c%d" % ex, align_bytes=64)
-            s_tile = keep.tile([P, 512], U8, name="w1_s%d" % ex, align_bytes=64)
-            cod[("w1", ex)] = c_tile
-            sca[("w1", ex)] = s_tile
-        for q in range(4):
-            c_tile = keep.tile([P, 256], U32, name="w2_c%d" % q, align_bytes=64)
-            s_tile = keep.tile([P, 256], U8, name="w2_s%d" % q, align_bytes=64)
-            cod[("w2", q)] = c_tile
-            sca[("w2", q)] = s_tile
-        live_banks = {}
-
-        def job_t(kind, idx, b, pool_tag="tp"):
-            if kind == "w1" and b == 0:
-                g_tile = work.tile([P, 512 * 4], BF16, name="w1_g", tag="w1_g", align_bytes=64)
-                grp[(kind, idx)] = g_tile
-            if kind == "w2":
-                g_tile = work.tile([P, 256 * 4], BF16, name="w2_g", tag="w2_g", bufs=2, align_bytes=64)
-                grp[(kind, idx)] = g_tile
-            if kind == "h":
-                src_tile = h_sb[2 * idx + b]
-            elif kind == "w1":
-                src_tile = w1_sb[2 * idx + b]
-            else:
-                src_tile = w2_sb[idx]
-            live_banks[(kind, idx, b)] = t_bank(src_tile, pool_tag)
-
-        def job_x(kind, idx, b, engine):
-            x_bank(live_banks[(kind, idx, b)], grp[(kind, idx)][:, b * 1024:(b + 1) * 1024], engine)
-
-        def job_q(kind, idx, lo=0, hi=None):
-            width = cod[(kind, idx)].shape[1]
-            top = width if hi is None else hi
-            quantise(grp[(kind, idx)][:, 4 * lo:4 * top], cod[(kind, idx)][:, lo:top], sca[(kind, idx)][:, lo:top])
-
-        s1_banks = {}
-        planes = {}
-        h1_g = {}
-        h1_c = {}
-        h1_s = {}
-        s2_bank = {}
-        y_sb = {}
-        acc = []
-        for half in range(2):
-            acc_tile = keep.tile([P, HALF_MT, NACT], F32, name="acc%d" % half)
-            acc.append(acc_tile)
-        out1_view = out_1.rearrange("(p mt) x a -> p mt x a", mt=MT)
-        out0_view = out_0.rearrange("(p mt) a -> p mt a", mt=MT)
-
-        def mm1(n, ts=(0, 1, 2, 3)):
-            ex, half = n // 2, n % 2
-            if n not in s1_banks:
-                s1_banks[n] = {}
-                pl_tile = work.tile([P, 4, 512], BF16, name="planes", tag="planes")
-                planes[n] = pl_tile
-            for t in ts:
-                bank = ps_s1.tile([P, 512], F32, name="s1_bank", tag="s1")
-                nc.tensor.matmul_mx(
-                    out=bank[:],
-                    lhsT=cod[("w1", ex)][:, t * P:(t + 1) * P].bitcast(FP8X4),
-                    lhsT_scale=sca[("w1", ex)][:, t * P:(t + 1) * P],
-                    rhs=cod[("h", half)][:].bitcast(FP8X4),
-                    rhs_scale=sca[("h", half)][:],
-                    start=True,
-                    stop=True,
+        def prepare(name, pairs, copies):
+            columns = 2 * P * len(pairs)
+            grouped = rotating.tile([P, PACK * columns], BF16, name="grouped", tag="grouped%d" % columns, align_bytes=64)
+            for b in range(len(pairs)):
+                bank = psum_transposes.tile([P, 2, 2, P], F32, name="bank", tag="bank")
+                for s in range(2):
+                    words = pairs[b][:, s, :].bitcast(F32)
+                    for u in range(2):
+                        nc.tensor.transpose(bank[:, s, u, :], words[:, u * P:(u + 1) * P], identity[:])
+                part = grouped[:, PACK * 2 * P * b:PACK * 2 * P * (b + 1)]
+                copies[b](
+                    out=part.bitcast(F32).rearrange("p (s c u) -> p s c u", s=2, u=2),
+                    in_=bank[:].rearrange("p s u c -> p s c u"),
                 )
-                s1_banks[n][t] = bank
+            codes = resident.tile([P, columns], U32, name="%s_codes" % name, align_bytes=64)
+            scales = resident.tile([P, columns], U8, name="%s_scales" % name, align_bytes=64)
+            nc.vector.quantize_mx(out=codes[:].bitcast(FP8X4), scales=scales[:], in_=grouped[:])
+            return codes, scales
 
-        def c1(n, t):
-            ex = n // 2
-            bias = b1T[:, 4 * ex + t:4 * ex + t + 1]
-            if t in V_PLANES.get(n, ()):
-                nc.vector.tensor_scalar(
-                    out=planes[n][:, t, :], in0=s1_banks[n][t][:], scalar1=bias, scalar2=0.0, op0=ALU.add, op1=ALU.max
-                )
-            else:
-                nc.scalar.activation(out=planes[n][:, t, :], in_=s1_banks[n][t][:], func=ACT.Relu, bias=bias, scale=1.0)
+        by_vector = nc.vector.tensor_copy
+        by_scalar = nc.scalar.copy
 
-        def regroup(n, engine):
-            if n not in h1_g:
-                g_tile = work.tile([P, 512 * 4], BF16, name="h1_g", tag="h1_g", align_bytes=64)
-                h1_g[n] = g_tile
-            cut = 512 - S_COLS[n]
-            lo, hi = (0, cut) if engine == "v" else (cut, 512)
-            if lo == hi:
-                return
-            dst = h1_g[n][:, 4 * lo:4 * hi].rearrange("p (c i t) -> p c t i", i=4, t=4)
-            src = planes[n][:, :, lo:hi].rearrange("p t (c i) -> p c t i", i=4)
-            if engine == "v":
-                nc.vector.tensor_copy(out=dst, in_=src)
-            else:
-                nc.scalar.copy(out=dst, in_=src)
+        h_mx = {}
+        w1_mx = {}
+        w2_mx = {}
+        h_mx[0] = prepare("h0", h_raw[0], [by_vector, by_scalar])
+        w1_mx[0] = prepare("w1_0", w1_raw[0], [by_vector, by_scalar])
+        h_mx[1] = prepare("h1", h_raw[1], [by_vector, by_vector])
+        w2_mx[0] = prepare("w2_0", w2_raw[0], [by_vector])
 
-        def q1(n, lo=0, hi=512):
-            if n not in h1_c:
-                c_tile = work.tile([P, 512], U32, name="h1_c", tag="h1_c", align_bytes=64)
-                s_tile = work.tile([P, 512], U8, name="h1_s", tag="h1_s", align_bytes=64)
-                h1_c[n] = c_tile
-                h1_s[n] = s_tile
-            quantise(h1_g[n][:, 4 * lo:4 * hi], h1_c[n][:, lo:hi], h1_s[n][:, lo:hi])
+        gated_sum = [resident.tile([P, HALF_TILES, ACTIONS], F32, name="gated_sum%d" % half) for half in range(2)]
+        out_0_view = out_0.rearrange("(p r) a -> p r a", r=ROW_TILES)
+        out_1_view = out_1.rearrange("(p r) x a -> p r x a", r=ROW_TILES)
 
-        def mm2(n, tiles=(0, 1, 2, 3)):
-            ex = n // 2
-            if n not in s2_bank:
-                bank = ps_s2.tile([P, HALF_MT, NACT], F32, name="s2_bank", tag="s2")
-                s2_bank[n] = bank
-            lo = (ex % 2) * NACT
-            for i in tiles:
-                nc.tensor.matmul_mx(
-                    out=s2_bank[n][:, i, :],
-                    lhsT=h1_c[n][:, i * P:(i + 1) * P].bitcast(FP8X4),
-                    lhsT_scale=h1_s[n][:, i * P:(i + 1) * P],
-                    rhs=cod[("w2", ex // 2)][:, lo:lo + NACT].bitcast(FP8X4),
-                    rhs_scale=sca[("w2", ex // 2)][:, lo:lo + NACT],
-                    start=True,
-                    stop=True,
-                )
+        for x in range(EXPERTS):
+            if x + 1 < EXPERTS:
+                w1_mx[x + 1] = prepare("w1_%d" % (x + 1), w1_raw[x + 1], [by_vector, by_vector] if x == 0 else [by_scalar, by_scalar])
+            if x % 2 == 0 and x + 2 < EXPERTS:
+                w2_mx[x // 2 + 1] = prepare("w2_%d" % (x // 2 + 1), w2_raw[x // 2 + 1], [by_scalar])
+            w1_codes, w1_scales = w1_mx[x]
+            w2_codes, w2_scales = w2_mx[x // 2]
+            w2_columns = slice((x % 2) * ACTIONS, (x % 2 + 1) * ACTIONS)
 
-        def add_b2(n):
-            ex = n // 2
-            y_tile = work.tile([P, HALF_MT, NACT], F32, name="y_sb", tag="y_sb", bufs=4)
-            y_sb[n] = y_tile
-            nc.vector.tensor_tensor(
-                out=y_tile[:],
-                in0=s2_bank[n][:],
-                in1=b2bc[:, ex * NACT:(ex + 1) * NACT].unsqueeze(1).to_broadcast([P, HALF_MT, NACT]),
-                op=ALU.add,
-            )
+            for half in range(2):
+                h_codes, h_scales = h_mx[half]
+                tiles = slice(half * HALF_TILES, (half + 1) * HALF_TILES)
 
-        def gate_sum(n):
-            ex, half = n // 2, n % 2
-            for i in range(HALF_MT):
-                col = (half * HALF_MT + i) * NEXP + ex
-                if ex == 0:
-                    nc.vector.tensor_scalar(
-                        out=acc[half][:, i, :], in0=y_sb[n][:, i, :], scalar1=gate[:, col:col + 1], scalar2=None, op0=ALU.mult
+                planes = rotating.tile([P, PACK, HALF_ROWS], BF16, name="planes")
+                for t in range(PACK):
+                    plane_bank = psum_planes.tile([P, HALF_ROWS], F32, name="plane_bank")
+                    nc.tensor.matmul_mx(
+                        out=plane_bank[:],
+                        lhsT=w1_codes[:, t * P:(t + 1) * P].bitcast(FP8X4),
+                        lhsT_scale=w1_scales[:, t * P:(t + 1) * P],
+                        rhs=h_codes[:].bitcast(FP8X4),
+                        rhs_scale=h_scales[:],
+                        start=True,
+                        stop=True,
                     )
-                else:
-                    nc.vector.scalar_tensor_tensor(
-                        out=acc[half][:, i, :],
-                        in0=y_sb[n][:, i, :],
-                        scalar=gate[:, col:col + 1],
-                        in1=acc[half][:, i, :],
-                        op0=ALU.mult,
-                        op1=ALU.add,
+                    nc.scalar.activation(
+                        out=planes[:, t, :],
+                        in_=plane_bank[:],
+                        func=ACT.Relu,
+                        bias=b1[:, PACK * x + t:PACK * x + t + 1],
+                        scale=1.0,
                     )
 
-        def store(n):
-            ex, half = n // 2, n % 2
-            nc.sync.dma_start(out=out1_view[:, half * HALF_MT:(half + 1) * HALF_MT, ex, :], in_=y_sb[n][:])
-            if ex == NEXP - 1:
-                nc.sync.dma_start(out=out0_view[:, half * HALF_MT:(half + 1) * HALF_MT, :], in_=acc[half][:])
+                h1_grouped = rotating.tile([P, PACK * HALF_ROWS], BF16, name="h1_grouped", align_bytes=64)
+                cut = HALF_ROWS - scalar_share(2 * x + half)
+                for copy, lo, hi in ((by_scalar, cut, HALF_ROWS), (by_vector, 0, cut)):
+                    copy(
+                        out=h1_grouped[:, PACK * lo:PACK * hi].rearrange("p (c i t) -> p c t i", i=4, t=PACK),
+                        in_=planes[:, :, lo:hi].rearrange("p t (c i) -> p c t i", i=4),
+                    )
+                h1_codes = rotating.tile([P, HALF_ROWS], U32, name="h1_codes", align_bytes=64)
+                h1_scales = rotating.tile([P, HALF_ROWS], U8, name="h1_scales", align_bytes=64)
+                nc.vector.quantize_mx(out=h1_codes[:].bitcast(FP8X4), scales=h1_scales[:], in_=h1_grouped[:])
 
-        job_t("h", 0, 0)
-        job_t("h", 0, 1)
-        job_x("h", 0, 0, "v")
-        job_x("h", 0, 1, "s")
-        job_t("w1", 0, 0)
-        job_t("w1", 0, 1)
-        job_q("h", 0, 0, 256)
-        job_x("w1", 0, 0, "v")
-        job_x("w1", 0, 1, "s")
-        job_q("h", 0, 256, 512)
-        job_q("w1", 0, 0, 256)
-        job_q("w1", 0, 256, 512)
-        job_t("h", 1, 0)
-        mm1(0, (0, 1))
-        job_t("h", 1, 1)
-        mm1(0, (2, 3))
-        job_x("h", 1, 0, "v")
-        job_x("h", 1, 1, "v")
-        job_q("h", 1)
-        for t in range(4):
-            c1(0, t)
-        regroup(0, "s")
-        job_t("w1", 1, 0)
-        job_t("w1", 1, 1)
-        job_x("w1", 1, 0, "v")
-        job_x("w1", 1, 1, "v")
+                y_bank = psum_stage2.tile([P, HALF_TILES, ACTIONS], F32, name="y_bank")
+                for i in range(HALF_TILES):
+                    nc.tensor.matmul_mx(
+                        out=y_bank[:, i, :],
+                        lhsT=h1_codes[:, i * P:(i + 1) * P].bitcast(FP8X4),
+                        lhsT_scale=h1_scales[:, i * P:(i + 1) * P],
+                        rhs=w2_codes[:, w2_columns].bitcast(FP8X4),
+                        rhs_scale=w2_scales[:, w2_columns],
+                        start=True,
+                        stop=True,
+                    )
+                y = rotating.tile([P, HALF_TILES, ACTIONS], F32, name="y", bufs=4)
+                nc.vector.tensor_tensor(
+                    out=y[:],
+                    in0=y_bank[:],
+                    in1=b2_all[:, x * ACTIONS:(x + 1) * ACTIONS].unsqueeze(1).to_broadcast([P, HALF_TILES, ACTIONS]),
+                    op=ALU.add,
+                )
+                nc.sync.dma_start(out=out_1_view[:, tiles, x, :], in_=y[:])
 
-        prep_plan = {
-            1: [("b2", 0, "ss")],
-            2: [("w1", 2, "ss")],
-            3: [("w2", 1, "s")],
-            4: [("w1", 3, "ss")],
-            5: [("w2", 2, "s")],
-            6: [("w1", 4, "ss")],
-            7: [("w2", 3, "s")],
-            8: [("w1", 5, "ss")],
-            10: [("w1", 6, "ss")],
-            12: [("w1", 7, "ss")],
-        }
-
-        for k in range(1, UNITS + 2):
-            jobs = prep_plan.get(k, [])
-            if k < UNITS:
-                mm1(k)
-            if k >= 2:
-                mm2(k - 2)
-            if k < UNITS:
-                for t in range(4):
-                    c1(k, t)
-                regroup(k, "s")
-            for kind, idx, engines in jobs:
-                if kind == "b2":
-                    spread_b2(0, engines[0])
-                    spread_b2(1, engines[1])
-                else:
-                    for b in range(len(engines)):
-                        job_t(kind, idx, b)
-                    for b in range(len(engines)):
-                        job_x(kind, idx, b, engines[b])
-            if 1 <= k <= UNITS:
-                regroup(k - 1, "v")
-            if k == 1:
-                job_q("w1", 1)
-                job_t("w2", 0, 0)
-                job_x("w2", 0, 0, "v")
-            for kind, idx, engines in prep_plan.get(k - 1, []):
-                if kind != "b2":
-                    job_q(kind, idx)
-            if k >= 2:
-                add_b2(k - 2)
-            if 1 <= k <= UNITS:
-                q1(k - 1)
-            if k == 1:
-                job_q("w2", 0)
-            if k >= 2:
-                gate_sum(k - 2)
-                store(k - 2)
+                for i in range(HALF_TILES):
+                    column = (half * HALF_TILES + i) * EXPERTS + x
+                    if x == 0:
+                        nc.vector.tensor_scalar(
+                            out=gated_sum[half][:, i, :], in0=y[:, i, :], scalar1=gate[:, column:column + 1], scalar2=None, op0=ALU.mult
+                        )
+                    else:
+                        nc.vector.scalar_tensor_tensor(
+                            out=gated_sum[half][:, i, :],
+                            in0=y[:, i, :],
+                            scalar=gate[:, column:column + 1],
+                            in1=gated_sum[half][:, i, :],
+                            op0=ALU.mult,
+                            op1=ALU.add,
+                        )
+                if x == EXPERTS - 1:
+                    nc.sync.dma_start(out=out_0_view[:, tiles, :], in_=gated_sum[half][:])

@@ -43,6 +43,9 @@ def tile_mspagent_pb_kernel(tc, h, gate_logit, e_w1, e_b1, e_w2, e_b2, out_0, ou
         b1_rows = resident.tile([P, 2 * P], BF16, name="b1_rows")
         nc.vector.memset(b1_rows[:], 0.0)
         nc.sync.dma_start(out=b1_rows[0:2 * EXPERTS, :], in_=e_b1.rearrange("x (u c) -> (x u) c", u=2))
+        b2_row = resident.tile([P, EXPERTS * ACTIONS], BF16, name="b2_row")
+        nc.vector.memset(b2_row[:], 0.0)
+        nc.sync.dma_start(out=b2_row[0:1, :], in_=e_b2.rearrange("(o x) a -> o (x a)", o=1))
 
         def load_pair(name, view):
             pair = resident.tile([P, 2, HID], BF16, name=name)
@@ -72,8 +75,6 @@ def tile_mspagent_pb_kernel(tc, h, gate_logit, e_w1, e_b1, e_w2, e_b2, out_0, ou
         h_raw[1] = load_h(1)
         w1_raw[1] = load_w1(1)
         w2_raw[0] = load_w2(0)
-        b2_all = resident.tile([P, EXPERTS * ACTIONS], BF16, name="b2_all")
-        nc.sync.dma_start(out=b2_all[:], in_=e_b2.rearrange("x a -> (x a)").partition_broadcast(P))
         for x in range(2, EXPERTS):
             w1_raw[x] = load_w1(x)
             if x - 1 < EXPERTS // 2:
@@ -120,6 +121,14 @@ def tile_mspagent_pb_kernel(tc, h, gate_logit, e_w1, e_b1, e_w2, e_b2, out_0, ou
         w1_mx[0] = prepare("w1_0", w1_raw[0], [by_vector, by_scalar])
         h_mx[1] = prepare("h1", h_raw[1], [by_vector, by_vector])
         w2_mx[0] = prepare("w2_0", w2_raw[0], [by_vector])
+
+        ones = resident.tile([P, P], BF16, name="ones")
+        nc.vector.memset(ones[:], 1.0)
+        b2_all = resident.tile([P, EXPERTS * ACTIONS], F32, name="b2_all")
+        for c in range(EXPERTS * ACTIONS // HALF_ROWS):
+            b2_bank = psum_stage2.tile([P, HALF_ROWS], F32, name="b2_bank", tag="y_bank")
+            nc.tensor.matmul(out=b2_bank[:], lhsT=ones[:], rhs=b2_row[:, c * HALF_ROWS:(c + 1) * HALF_ROWS], start=True, stop=True)
+            nc.vector.tensor_copy(out=b2_all[:, c * HALF_ROWS:(c + 1) * HALF_ROWS], in_=b2_bank[:])
 
         gated_sum = [resident.tile([P, HALF_TILES, ACTIONS], F32, name="gated_sum%d" % half) for half in range(2)]
         out_0_view = out_0.rearrange("(p r) a -> p r a", r=ROW_TILES)

@@ -92,126 +92,171 @@ def tile_mspagent_pb_kernel(tc, h, gate_logit, e_w1, e_b1, e_w2, e_b2, out_0, ou
         b1 = resident.tile([P, PACK * EXPERTS], F32, name="b1")
         nc.vector.tensor_copy(out=b1[:], in_=b1_bank[:, 0, 0, :].bitcast(BF16)[:, 0:PACK * EXPERTS])
 
-        def prepare(name, pairs, copies):
-            columns = 2 * P * len(pairs)
-            grouped = rotating.tile([P, PACK * columns], BF16, name="grouped", tag="grouped%d" % columns, align_bytes=64)
-            for b in range(len(pairs)):
-                bank = psum_transposes.tile([P, 2, 2, P], F32, name="bank", tag="bank")
-                for s in range(2):
-                    words = pairs[b][:, s, :].bitcast(F32)
-                    for u in range(2):
-                        nc.tensor.transpose(bank[:, s, u, :], words[:, u * P:(u + 1) * P], identity[:])
-                part = grouped[:, PACK * 2 * P * b:PACK * 2 * P * (b + 1)]
-                copies[b](
-                    out=part.bitcast(F32).rearrange("p (s c u) -> p s c u", s=2, u=2),
-                    in_=bank[:].rearrange("p s u c -> p s c u"),
-                )
-            codes = resident.tile([P, columns], U32, name="%s_codes" % name, align_bytes=64)
-            scales = resident.tile([P, columns], U8, name="%s_scales" % name, align_bytes=64)
-            nc.vector.quantize_mx(out=codes[:].bitcast(FP8X4), scales=scales[:], in_=grouped[:])
-            return codes, scales
-
-        by_vector = nc.vector.tensor_copy
-        by_scalar = nc.scalar.copy
-
-        h_mx = {}
-        w1_mx = {}
-        w2_mx = {}
-        h_mx[0] = prepare("h0", h_raw[0], [by_vector, by_scalar])
-        w1_mx[0] = prepare("w1_0", w1_raw[0], [by_vector, by_scalar])
-        h_mx[1] = prepare("h1", h_raw[1], [by_vector, by_vector])
-        w2_mx[0] = prepare("w2_0", w2_raw[0], [by_vector])
-
         ones = resident.tile([P, P], BF16, name="ones")
         nc.vector.memset(ones[:], 1.0)
         b2_all = resident.tile([P, EXPERTS * ACTIONS], F32, name="b2_all")
         for c in range(EXPERTS * ACTIONS // HALF_ROWS):
             b2_bank = psum_stage2.tile([P, HALF_ROWS], F32, name="b2_bank", tag="y_bank")
             nc.tensor.matmul(out=b2_bank[:], lhsT=ones[:], rhs=b2_row[:, c * HALF_ROWS:(c + 1) * HALF_ROWS], start=True, stop=True)
-            nc.vector.tensor_copy(out=b2_all[:, c * HALF_ROWS:(c + 1) * HALF_ROWS], in_=b2_bank[:])
+            (nc.vector.tensor_copy, nc.scalar.copy)[c](out=b2_all[:, c * HALF_ROWS:(c + 1) * HALF_ROWS], in_=b2_bank[:])
+
+
+        by_vector = nc.vector.tensor_copy
+        by_scalar = nc.scalar.copy
+
+        def start_operand(name, pairs, copies):
+            columns = 2 * P * len(pairs)
+            grouped = rotating.tile([P, PACK * columns], BF16, name="grouped", tag="grouped%d" % columns, align_bytes=64)
+            banks = []
+            for pair in pairs:
+                bank = psum_transposes.tile([P, 2, 2, P], F32, name="bank", tag="bank")
+                for s in range(2):
+                    words = pair[:, s, :].bitcast(F32)
+                    for u in range(2):
+                        nc.tensor.transpose(bank[:, s, u, :], words[:, u * P:(u + 1) * P], identity[:])
+                banks.append(bank)
+            for b in range(len(pairs)):
+                part = grouped[:, PACK * 2 * P * b:PACK * 2 * P * (b + 1)]
+                copies[b](
+                    out=part.bitcast(F32).rearrange("p (s c u) -> p s c u", s=2, u=2),
+                    in_=banks[b][:].rearrange("p s u c -> p s c u"),
+                )
+            return name, grouped
+
+        mx = {}
+
+        def finish_operand(started):
+            name, grouped = started
+            columns = grouped.shape[1] // PACK
+            codes = resident.tile([P, columns], U32, name="%s_codes" % name, align_bytes=64)
+            scales = resident.tile([P, columns], U8, name="%s_scales" % name, align_bytes=64)
+            nc.vector.quantize_mx(out=codes[:].bitcast(FP8X4), scales=scales[:], in_=grouped[:])
+            mx[name] = (codes, scales)
 
         gated_sum = [resident.tile([P, HALF_TILES, ACTIONS], F32, name="gated_sum%d" % half) for half in range(2)]
         out_0_view = out_0.rearrange("(p r) a -> p r a", r=ROW_TILES)
         out_1_view = out_1.rearrange("(p r) x a -> p r x a", r=ROW_TILES)
+        live = {}
 
-        for x in range(EXPERTS):
-            if x + 1 < EXPERTS:
-                w1_mx[x + 1] = prepare("w1_%d" % (x + 1), w1_raw[x + 1], [by_vector, by_vector] if x == 0 else [by_scalar, by_scalar])
-            if x % 2 == 0 and x + 2 < EXPERTS:
-                w2_mx[x // 2 + 1] = prepare("w2_%d" % (x // 2 + 1), w2_raw[x // 2 + 1], [by_scalar])
-            w1_codes, w1_scales = w1_mx[x]
-            w2_codes, w2_scales = w2_mx[x // 2]
-            w2_columns = slice((x % 2) * ACTIONS, (x % 2 + 1) * ACTIONS)
-
-            for half in range(2):
-                h_codes, h_scales = h_mx[half]
-                tiles = slice(half * HALF_TILES, (half + 1) * HALF_TILES)
-
-                planes = rotating.tile([P, PACK, HALF_ROWS], BF16, name="planes")
-                for t in range(PACK):
-                    plane_bank = psum_planes.tile([P, HALF_ROWS], F32, name="plane_bank")
-                    nc.tensor.matmul_mx(
-                        out=plane_bank[:],
-                        lhsT=w1_codes[:, t * P:(t + 1) * P].bitcast(FP8X4),
-                        lhsT_scale=w1_scales[:, t * P:(t + 1) * P],
-                        rhs=h_codes[:].bitcast(FP8X4),
-                        rhs_scale=h_scales[:],
-                        start=True,
-                        stop=True,
-                    )
-                    nc.scalar.activation(
-                        out=planes[:, t, :],
-                        in_=plane_bank[:],
-                        func=ACT.Relu,
-                        bias=b1[:, PACK * x + t:PACK * x + t + 1],
-                        scale=1.0,
-                    )
-
-                h1_grouped = rotating.tile([P, PACK * HALF_ROWS], BF16, name="h1_grouped", align_bytes=64)
-                cut = HALF_ROWS - scalar_share(2 * x + half)
-                for copy, lo, hi in ((by_scalar, cut, HALF_ROWS), (by_vector, 0, cut)):
-                    copy(
-                        out=h1_grouped[:, PACK * lo:PACK * hi].rearrange("p (c i t) -> p c t i", i=4, t=PACK),
-                        in_=planes[:, :, lo:hi].rearrange("p t (c i) -> p c t i", i=4),
-                    )
-                h1_codes = rotating.tile([P, HALF_ROWS], U32, name="h1_codes", align_bytes=64)
-                h1_scales = rotating.tile([P, HALF_ROWS], U8, name="h1_scales", align_bytes=64)
-                nc.vector.quantize_mx(out=h1_codes[:].bitcast(FP8X4), scales=h1_scales[:], in_=h1_grouped[:])
-
-                y_bank = psum_stage2.tile([P, HALF_TILES, ACTIONS], F32, name="y_bank")
-                for i in range(HALF_TILES):
-                    nc.tensor.matmul_mx(
-                        out=y_bank[:, i, :],
-                        lhsT=h1_codes[:, i * P:(i + 1) * P].bitcast(FP8X4),
-                        lhsT_scale=h1_scales[:, i * P:(i + 1) * P],
-                        rhs=w2_codes[:, w2_columns].bitcast(FP8X4),
-                        rhs_scale=w2_scales[:, w2_columns],
-                        start=True,
-                        stop=True,
-                    )
-                y = rotating.tile([P, HALF_TILES, ACTIONS], F32, name="y", bufs=4)
-                nc.vector.tensor_tensor(
-                    out=y[:],
-                    in0=y_bank[:],
-                    in1=b2_all[:, x * ACTIONS:(x + 1) * ACTIONS].unsqueeze(1).to_broadcast([P, HALF_TILES, ACTIONS]),
-                    op=ALU.add,
+        def stage1_passes(unit):
+            w1_codes, w1_scales = mx["w1_%d" % (unit // 2)]
+            h_codes, h_scales = mx["h_%d" % (unit % 2)]
+            for t in range(PACK):
+                plane_bank = psum_planes.tile([P, HALF_ROWS], F32, name="plane_bank")
+                nc.tensor.matmul_mx(
+                    out=plane_bank[:],
+                    lhsT=w1_codes[:, t * P:(t + 1) * P].bitcast(FP8X4),
+                    lhsT_scale=w1_scales[:, t * P:(t + 1) * P],
+                    rhs=h_codes[:].bitcast(FP8X4),
+                    rhs_scale=h_scales[:],
+                    start=True,
+                    stop=True,
                 )
-                nc.sync.dma_start(out=out_1_view[:, tiles, x, :], in_=y[:])
+                live[("plane_bank", unit, t)] = plane_bank
 
-                for i in range(HALF_TILES):
-                    column = (half * HALF_TILES + i) * EXPERTS + x
-                    if x == 0:
-                        nc.vector.tensor_scalar(
-                            out=gated_sum[half][:, i, :], in0=y[:, i, :], scalar1=gate[:, column:column + 1], scalar2=None, op0=ALU.mult
-                        )
-                    else:
-                        nc.vector.scalar_tensor_tensor(
-                            out=gated_sum[half][:, i, :],
-                            in0=y[:, i, :],
-                            scalar=gate[:, column:column + 1],
-                            in1=gated_sum[half][:, i, :],
-                            op0=ALU.mult,
-                            op1=ALU.add,
-                        )
-                if x == EXPERTS - 1:
-                    nc.sync.dma_start(out=out_0_view[:, tiles, :], in_=gated_sum[half][:])
+        def regroup(unit, copy, lo, hi):
+            copy(
+                out=live[("h1_grouped", unit)][:, PACK * lo:PACK * hi].rearrange("p (c i t) -> p c t i", i=4, t=PACK),
+                in_=live[("planes", unit)][:, :, lo:hi].rearrange("p t (c i) -> p c t i", i=4),
+            )
+
+        def planes_out(unit):
+            planes = rotating.tile([P, PACK, HALF_ROWS], BF16, name="planes")
+            live[("planes", unit)] = planes
+            for t in range(PACK):
+                column = PACK * (unit // 2) + t
+                nc.scalar.activation(
+                    out=planes[:, t, :], in_=live[("plane_bank", unit, t)][:], func=ACT.Relu, bias=b1[:, column:column + 1], scale=1.0
+                )
+            h1_grouped = rotating.tile([P, PACK * HALF_ROWS], BF16, name="h1_grouped", align_bytes=64)
+            live[("h1_grouped", unit)] = h1_grouped
+            regroup(unit, by_scalar, HALF_ROWS - scalar_share(unit), HALF_ROWS)
+
+        def quantise_h1(unit):
+            h1_codes = rotating.tile([P, HALF_ROWS], U32, name="h1_codes", align_bytes=64)
+            h1_scales = rotating.tile([P, HALF_ROWS], U8, name="h1_scales", align_bytes=64)
+            nc.vector.quantize_mx(out=h1_codes[:].bitcast(FP8X4), scales=h1_scales[:], in_=live[("h1_grouped", unit)][:])
+            live[("h1_mx", unit)] = (h1_codes, h1_scales)
+
+        def stage2_passes(unit):
+            x = unit // 2
+            h1_codes, h1_scales = live[("h1_mx", unit)]
+            w2_codes, w2_scales = mx["w2_%d" % (x // 2)]
+            first = (x % 2) * ACTIONS
+            y_bank = psum_stage2.tile([P, HALF_TILES, ACTIONS], F32, name="y_bank")
+            live[("y_bank", unit)] = y_bank
+            for i in range(HALF_TILES):
+                nc.tensor.matmul_mx(
+                    out=y_bank[:, i, :],
+                    lhsT=h1_codes[:, i * P:(i + 1) * P].bitcast(FP8X4),
+                    lhsT_scale=h1_scales[:, i * P:(i + 1) * P],
+                    rhs=w2_codes[:, first:first + ACTIONS].bitcast(FP8X4),
+                    rhs_scale=w2_scales[:, first:first + ACTIONS],
+                    start=True,
+                    stop=True,
+                )
+
+        def add_b2(unit):
+            x = unit // 2
+            y = rotating.tile([P, HALF_TILES, ACTIONS], F32, name="y", bufs=4)
+            live[("y", unit)] = y
+            nc.vector.tensor_tensor(
+                out=y[:],
+                in0=live[("y_bank", unit)][:],
+                in1=b2_all[:, x * ACTIONS:(x + 1) * ACTIONS].unsqueeze(1).to_broadcast([P, HALF_TILES, ACTIONS]),
+                op=ALU.add,
+            )
+
+        def gate_and_store(unit):
+            x, half = unit // 2, unit % 2
+            y = live[("y", unit)]
+            for i in range(HALF_TILES):
+                column = (half * HALF_TILES + i) * EXPERTS + x
+                if x == 0:
+                    nc.vector.tensor_scalar(
+                        out=gated_sum[half][:, i, :], in0=y[:, i, :], scalar1=gate[:, column:column + 1], scalar2=None, op0=ALU.mult
+                    )
+                else:
+                    nc.vector.scalar_tensor_tensor(
+                        out=gated_sum[half][:, i, :],
+                        in0=y[:, i, :],
+                        scalar=gate[:, column:column + 1],
+                        in1=gated_sum[half][:, i, :],
+                        op0=ALU.mult,
+                        op1=ALU.add,
+                    )
+            tiles = slice(half * HALF_TILES, (half + 1) * HALF_TILES)
+            nc.sync.dma_start(out=out_1_view[:, tiles, x, :], in_=y[:])
+            if x == EXPERTS - 1:
+                nc.sync.dma_start(out=out_0_view[:, tiles, :], in_=gated_sum[half][:])
+
+        finish_operand(start_operand("h_0", h_raw[0], [by_vector, by_scalar]))
+        finish_operand(start_operand("w1_0", w1_raw[0], [by_vector, by_scalar]))
+        stage1_passes(0)
+        finish_operand(start_operand("h_1", h_raw[1], [by_vector, by_vector]))
+        planes_out(0)
+        started = [start_operand("w1_1", w1_raw[1], [by_vector, by_vector]), start_operand("w2_0", w2_raw[0], [by_vector])]
+
+        for k in range(1, UNITS + 2):
+            if k < UNITS:
+                stage1_passes(k)
+            if k >= 2:
+                stage2_passes(k - 2)
+            if k < UNITS:
+                planes_out(k)
+            to_finish = started
+            started = []
+            if k % 2 == 0 and k // 2 + 1 < EXPERTS:
+                started.append(start_operand("w1_%d" % (k // 2 + 1), w1_raw[k // 2 + 1], [by_scalar, by_scalar]))
+            if k % 2 == 1 and 1 <= k // 2 < EXPERTS // 2:
+                started.append(start_operand("w2_%d" % (k // 2), w2_raw[k // 2], [by_scalar]))
+            if k <= UNITS:
+                regroup(k - 1, by_vector, 0, HALF_ROWS - scalar_share(k - 1))
+            for operand in to_finish:
+                finish_operand(operand)
+            if k >= 2:
+                add_b2(k - 2)
+            if k <= UNITS:
+                quantise_h1(k - 1)
+            if k >= 2:
+                gate_and_store(k - 2)

from contextlib import ExitStack

import concourse.mybir as mybir
from concourse.masks import make_identity

F32 = mybir.dt.float32
BF16 = mybir.dt.bfloat16
U32 = mybir.dt.uint32
U8 = mybir.dt.uint8
FP8X4 = mybir.dt.float8_e4m3fn_x4
ACT = mybir.ActivationFunctionType
ALU = mybir.AluOpType

P = 128
PACK = 4
ROWS = 1024
HID = 512
ACTIONS = 128
EXPERTS = 8
ROW_TILES = ROWS // P
HALF_TILES = ROW_TILES // 2
HALF_ROWS = ROWS // 2
UNITS = 2 * EXPERTS

FLOPS = 2 * ROWS * HID * HID * EXPERTS + 2 * ROWS * HID * ACTIONS * EXPERTS


def scalar_share(unit):
    return 32 * 2 ** max(0, unit - (UNITS - 4))


def tile_mspagent_pb_kernel(tc, h, gate_logit, e_w1, e_b1, e_w2, e_b2, out_0, out_1):
    nc = tc.nc
    with ExitStack() as ctx:
        resident = ctx.enter_context(tc.tile_pool(name="resident", bufs=1))
        rotating = ctx.enter_context(tc.tile_pool(name="rotating", bufs=3))
        psum_planes = ctx.enter_context(tc.psum_pool(name="psum_planes", bufs=4))
        psum_transposes = ctx.enter_context(tc.psum_pool(name="psum_transposes", bufs=2))
        psum_stage2 = ctx.enter_context(tc.psum_pool(name="psum_stage2", bufs=2))

        gate_logits = resident.tile([P, ROW_TILES * EXPERTS], BF16, name="gate_logits")
        nc.sync.dma_start(out=gate_logits[:], in_=gate_logit.rearrange("(p r) x -> p (r x)", r=ROW_TILES))
        b1_rows = resident.tile([P, 2 * P], BF16, name="b1_rows")
        nc.vector.memset(b1_rows[:], 0.0)
        nc.sync.dma_start(out=b1_rows[0:2 * EXPERTS, :], in_=e_b1.rearrange("x (u c) -> (x u) c", u=2))
        b2_row = resident.tile([P, EXPERTS * ACTIONS], BF16, name="b2_row")
        nc.vector.memset(b2_row[:], 0.0)
        nc.sync.dma_start(out=b2_row[0:1, :], in_=e_b2.rearrange("(o x) a -> o (x a)", o=1))

        def load_pair(name, view):
            pair = resident.tile([P, 2, HID], BF16, name=name)
            nc.sync.dma_start(out=pair[:], in_=view)
            return pair

        def load_h(half):
            view = h.rearrange("(p r) k -> p r k", r=ROW_TILES)
            first = half * HALF_TILES
            return [load_pair("h_%d_%d" % (half, b), view[:, first + 2 * b:first + 2 * b + 2, :]) for b in range(2)]

        def load_w1(x):
            return [
                load_pair("w1_%d_%d" % (x, u), e_w1[x, 2 * P * u:2 * P * (u + 1), :].rearrange("(p e) k -> p e k", e=2))
                for u in range(2)
            ]

        def load_w2(pair_of_experts):
            first = 2 * pair_of_experts
            return [load_pair("w2_%d" % pair_of_experts, e_w2[first:first + 2].rearrange("x a k -> a x k"))]

        h_raw = {}
        w1_raw = {}
        w2_raw = {}
        h_raw[0] = load_h(0)
        w1_raw[0] = load_w1(0)
        h_raw[1] = load_h(1)
        w1_raw[1] = load_w1(1)
        w2_raw[0] = load_w2(0)
        for x in range(2, EXPERTS):
            w1_raw[x] = load_w1(x)
            if x - 1 < EXPERTS // 2:
                w2_raw[x - 1] = load_w2(x - 1)

        identity = resident.tile([P, P], F32, name="identity")
        make_identity(nc, identity[:])

        gate = resident.tile([P, ROW_TILES * EXPERTS], F32, name="gate")
        nc.scalar.activation(out=gate[:], in_=gate_logits[:], func=ACT.Sigmoid)
        nc.vector.tensor_scalar(out=gate[:], in0=gate[:], scalar1=1.0 / EXPERTS, scalar2=None, op0=ALU.mult)

        b1_bank = psum_transposes.tile([P, 2, 2, P], F32, name="b1_bank", tag="bank")
        nc.tensor.transpose(b1_bank[:, 0, 0, :], b1_rows[:].bitcast(F32), identity[:])
        b1 = resident.tile([P, PACK * EXPERTS], F32, name="b1")
        nc.vector.tensor_copy(out=b1[:], in_=b1_bank[:, 0, 0, :].bitcast(BF16)[:, 0:PACK * EXPERTS])

        ones = resident.tile([P, P], BF16, name="ones")
        nc.vector.memset(ones[:], 1.0)
        b2_all = resident.tile([P, EXPERTS * ACTIONS], F32, name="b2_all")
        for c in range(EXPERTS * ACTIONS // HALF_ROWS):
            b2_bank = psum_stage2.tile([P, HALF_ROWS], F32, name="b2_bank", tag="y_bank")
            nc.tensor.matmul(out=b2_bank[:], lhsT=ones[:], rhs=b2_row[:, c * HALF_ROWS:(c + 1) * HALF_ROWS], start=True, stop=True)
            (nc.vector.tensor_copy, nc.scalar.copy)[c](out=b2_all[:, c * HALF_ROWS:(c + 1) * HALF_ROWS], in_=b2_bank[:])


        by_vector = nc.vector.tensor_copy
        by_scalar = nc.scalar.copy

        def start_operand(name, pairs, copies):
            columns = 2 * P * len(pairs)
            grouped = rotating.tile([P, PACK * columns], BF16, name="grouped", tag="grouped%d" % columns, align_bytes=64)
            banks = []
            for pair in pairs:
                bank = psum_transposes.tile([P, 2, 2, P], F32, name="bank", tag="bank")
                for s in range(2):
                    words = pair[:, s, :].bitcast(F32)
                    for u in range(2):
                        nc.tensor.transpose(bank[:, s, u, :], words[:, u * P:(u + 1) * P], identity[:])
                banks.append(bank)
            for b in range(len(pairs)):
                part = grouped[:, PACK * 2 * P * b:PACK * 2 * P * (b + 1)]
                copies[b](
                    out=part.bitcast(F32).rearrange("p (s c u) -> p s c u", s=2, u=2),
                    in_=banks[b][:].rearrange("p s u c -> p s c u"),
                )
            return name, grouped

        mx = {}

        def finish_operand(started):
            name, grouped = started
            columns = grouped.shape[1] // PACK
            codes = resident.tile([P, columns], U32, name="%s_codes" % name, align_bytes=64)
            scales = resident.tile([P, columns], U8, name="%s_scales" % name, align_bytes=64)
            nc.vector.quantize_mx(out=codes[:].bitcast(FP8X4), scales=scales[:], in_=grouped[:])
            mx[name] = (codes, scales)

        gated_sum = [resident.tile([P, HALF_TILES, ACTIONS], F32, name="gated_sum%d" % half) for half in range(2)]
        out_0_view = out_0.rearrange("(p r) a -> p r a", r=ROW_TILES)
        out_1_view = out_1.rearrange("(p r) x a -> p r x a", r=ROW_TILES)
        live = {}

        def stage1_passes(unit):
            w1_codes, w1_scales = mx["w1_%d" % (unit // 2)]
            h_codes, h_scales = mx["h_%d" % (unit % 2)]
            for t in range(PACK):
                plane_bank = psum_planes.tile([P, HALF_ROWS], F32, name="plane_bank")
                nc.tensor.matmul_mx(
                    out=plane_bank[:],
                    lhsT=w1_codes[:, t * P:(t + 1) * P].bitcast(FP8X4),
                    lhsT_scale=w1_scales[:, t * P:(t + 1) * P],
                    rhs=h_codes[:].bitcast(FP8X4),
                    rhs_scale=h_scales[:],
                    start=True,
                    stop=True,
                )
                live[("plane_bank", unit, t)] = plane_bank

        def regroup(unit, copy, lo, hi):
            copy(
                out=live[("h1_grouped", unit)][:, PACK * lo:PACK * hi].rearrange("p (c i t) -> p c t i", i=4, t=PACK),
                in_=live[("planes", unit)][:, :, lo:hi].rearrange("p t (c i) -> p c t i", i=4),
            )

        def planes_out(unit):
            planes = rotating.tile([P, PACK, HALF_ROWS], BF16, name="planes")
            live[("planes", unit)] = planes
            for t in range(PACK):
                column = PACK * (unit // 2) + t
                nc.scalar.activation(
                    out=planes[:, t, :], in_=live[("plane_bank", unit, t)][:], func=ACT.Relu, bias=b1[:, column:column + 1], scale=1.0
                )
            h1_grouped = rotating.tile([P, PACK * HALF_ROWS], BF16, name="h1_grouped", align_bytes=64)
            live[("h1_grouped", unit)] = h1_grouped
            regroup(unit, by_scalar, HALF_ROWS - scalar_share(unit), HALF_ROWS)

        def quantise_h1(unit):
            h1_codes = rotating.tile([P, HALF_ROWS], U32, name="h1_codes", align_bytes=64)
            h1_scales = rotating.tile([P, HALF_ROWS], U8, name="h1_scales", align_bytes=64)
            nc.vector.quantize_mx(out=h1_codes[:].bitcast(FP8X4), scales=h1_scales[:], in_=live[("h1_grouped", unit)][:])
            live[("h1_mx", unit)] = (h1_codes, h1_scales)

        def stage2_passes(unit):
            x = unit // 2
            h1_codes, h1_scales = live[("h1_mx", unit)]
            w2_codes, w2_scales = mx["w2_%d" % (x // 2)]
            first = (x % 2) * ACTIONS
            y_bank = psum_stage2.tile([P, HALF_TILES, ACTIONS], F32, name="y_bank")
            live[("y_bank", unit)] = y_bank
            for i in range(HALF_TILES):
                nc.tensor.matmul_mx(
                    out=y_bank[:, i, :],
                    lhsT=h1_codes[:, i * P:(i + 1) * P].bitcast(FP8X4),
                    lhsT_scale=h1_scales[:, i * P:(i + 1) * P],
                    rhs=w2_codes[:, first:first + ACTIONS].bitcast(FP8X4),
                    rhs_scale=w2_scales[:, first:first + ACTIONS],
                    start=True,
                    stop=True,
                )

        def add_b2(unit):
            x = unit // 2
            y = rotating.tile([P, HALF_TILES, ACTIONS], F32, name="y", bufs=4)
            live[("y", unit)] = y
            nc.vector.tensor_tensor(
                out=y[:],
                in0=live[("y_bank", unit)][:],
                in1=b2_all[:, x * ACTIONS:(x + 1) * ACTIONS].unsqueeze(1).to_broadcast([P, HALF_TILES, ACTIONS]),
                op=ALU.add,
            )

        def gate_and_store(unit):
            x, half = unit // 2, unit % 2
            y = live[("y", unit)]
            for i in range(HALF_TILES):
                column = (half * HALF_TILES + i) * EXPERTS + x
                if x == 0:
                    nc.vector.tensor_scalar(
                        out=gated_sum[half][:, i, :], in0=y[:, i, :], scalar1=gate[:, column:column + 1], scalar2=None, op0=ALU.mult
                    )
                else:
                    nc.vector.scalar_tensor_tensor(
                        out=gated_sum[half][:, i, :],
                        in0=y[:, i, :],
                        scalar=gate[:, column:column + 1],
                        in1=gated_sum[half][:, i, :],
                        op0=ALU.mult,
                        op1=ALU.add,
                    )
            tiles = slice(half * HALF_TILES, (half + 1) * HALF_TILES)
            nc.sync.dma_start(out=out_1_view[:, tiles, x, :], in_=y[:])
            if x == EXPERTS - 1:
                nc.sync.dma_start(out=out_0_view[:, tiles, :], in_=gated_sum[half][:])

        finish_operand(start_operand("h_0", h_raw[0], [by_vector, by_scalar]))
        finish_operand(start_operand("w1_0", w1_raw[0], [by_vector, by_scalar]))
        stage1_passes(0)
        finish_operand(start_operand("h_1", h_raw[1], [by_vector, by_vector]))
        planes_out(0)
        started = [start_operand("w1_1", w1_raw[1], [by_vector, by_vector]), start_operand("w2_0", w2_raw[0], [by_vector])]

        for k in range(1, UNITS + 2):
            if k < UNITS:
                stage1_passes(k)
            if k >= 2:
                stage2_passes(k - 2)
            if k < UNITS:
                planes_out(k)
            to_finish = started
            started = []
            if k % 2 == 0 and k // 2 + 1 < EXPERTS:
                started.append(start_operand("w1_%d" % (k // 2 + 1), w1_raw[k // 2 + 1], [by_scalar, by_scalar]))
            if k % 2 == 1 and 1 <= k // 2 < EXPERTS // 2:
                started.append(start_operand("w2_%d" % (k // 2), w2_raw[k // 2], [by_scalar]))
            if k <= UNITS:
                regroup(k - 1, by_vector, 0, HALF_ROWS - scalar_share(k - 1))
            for operand in to_finish:
                finish_operand(operand)
            if k >= 2:
                add_b2(k - 2)
            if k <= UNITS:
                quantise_h1(k - 1)
            if k >= 2:
                gate_and_store(k - 2)
